import numpy as np
import ml_dtypes


def mxq(x, axis, fmt="e4m3"):
    dtype, down = {"e4m3": (ml_dtypes.float8_e4m3fn, 7), "e5m2": (ml_dtypes.float8_e5m2, 14)}[fmt]
    v = np.moveaxis(np.asarray(x, np.float32).astype(ml_dtypes.bfloat16).astype(np.float64), axis, -1)
    blocks = v.reshape(v.shape[:-1] + (-1, 32))
    amax = np.abs(blocks).max(-1, keepdims=True)
    byte = np.maximum(np.where(amax > 0, np.frexp(amax)[1] - 1 + 127, 0) - down, 1)
    scale = np.exp2(byte - 127.0)
    codes = (blocks / scale).astype(np.float32).astype(dtype).astype(np.float64)
    return np.moveaxis((codes * scale).reshape(v.shape), -1, axis)


WIDE = False


def mx_kscale(k):
    if not WIDE:
        return np.ones(k)
    levels = np.array([18, -18])
    if k % 512:
        return np.exp2(np.random.permutation(np.resize(levels, k // 32))).repeat(32)
    a = np.empty((k // 512, 16))
    for p in range(k // 512):
        a[p, :8] = np.random.permutation(np.resize(levels, 8))
        for g in range(8):
            far = levels[np.abs(levels - a[p, g]) >= 10]
            a[p, g + 8] = far[np.random.randint(len(far))]
    return np.exp2(a.ravel()).repeat(32)


BF16 = ml_dtypes.bfloat16


def bf(x):
    return np.asarray(x, np.float32).astype(BF16)


def f64(x):
    return np.asarray(x).astype(np.float64)


B, T_IN, T_OUT, N, FEAT, HID, OUT, GRID_SIZE, SPLINE_ORDER = 2, 128, 128, 512, 8, 512, 512, 5, 3
M = B * N
KX = T_IN * FEAT
KY = T_OUT * FEAT
CAT = HID + HID
COEF = GRID_SIZE + SPLINE_ORDER
GRID_LO, GRID_HI = -1.0, 1.0


def sigmoid(v):
    return 1.0 / (1.0 + np.exp(-v))


def make_grid():
    step = (GRID_HI - GRID_LO) / GRID_SIZE
    return np.arange(-SPLINE_ORDER, GRID_SIZE + SPLINE_ORDER + 1) * step + GRID_LO


def b_splines(x, grid, order):
    x = x[..., None]
    bases = np.where((x >= grid[:-1]) & (x < grid[1:]), 1.0, 0.0)
    for k in range(1, order + 1):
        left = (x - grid[:-(k + 1)]) / (grid[k:-1] - grid[:-(k + 1)])
        right = (grid[k + 1:] - x) / (grid[k + 1:] - grid[1:-k])
        bases = left * bases[..., :-1] + right * bases[..., 1:]
    return bases


def b_splines_grad(x, grid):
    p = SPLINE_ORDER
    d = b_splines(x, grid, p - 1) * (p / (grid[p:] - grid[:-p]))
    return d[..., :-1] - d[..., 1:]


def setup_inputs():
    s = mx_kscale(M)
    u = mx_kscale(OUT)[:, None]
    v = mx_kscale(HID)
    vc = np.concatenate([v, np.ones(HID)])
    X0 = bf(np.random.standard_normal((B, T_IN, N, FEAT)))
    Y = bf(np.random.standard_normal((B, T_OUT, N, FEAT)))
    Wx0 = bf(np.random.standard_normal((HID, KX)) / np.sqrt(KX))
    bx = bf(np.random.standard_normal(HID) * 0.3)
    Wy = bf(np.random.standard_normal((HID, KY)) / np.sqrt(KY))
    by = bf(np.random.standard_normal(HID) * 0.3)
    base_w0 = bf(np.random.standard_normal((OUT, CAT)) * 3.0 / np.sqrt(CAT))
    spline_w = bf(np.random.standard_normal((OUT, CAT, COEF)))
    spline_scaler0 = bf(np.random.standard_normal((OUT, CAT)) * 1.5 / np.sqrt(CAT))
    g = bf(np.random.standard_normal((B, N, OUT)) * np.exp2(np.random.randint(-6, 1, (B, N, 1))) / s.reshape(B, N, 1) * u[:, 0])
    Xf = f64(X0).transpose(0, 2, 1, 3).reshape(M, KX)
    Hx = np.tanh(Xf @ f64(Wx0).T + f64(bx))
    return {
        "X": bf(f64(X0) * s.reshape(B, 1, N, 1)),
        "Y": Y,
        "Wx": bf(f64(Wx0) / v[:, None]),
        "bx": bx,
        "Wy": Wy,
        "by": by,
        "base_w": bf(f64(base_w0) * vc / u),
        "spline_w": spline_w,
        "spline_scaler": bf(f64(spline_scaler0) * vc / u),
        "Hx": np.asarray(Hx, np.float32),
        "grad_out": g,
    }


def reference(X, Y, Wx, bx, Wy, by, base_w, spline_w, spline_scaler, Hx, grad_out):
    Xf = f64(X).transpose(0, 2, 1, 3).reshape(M, KX)
    h = f64(Hx)
    g = f64(grad_out).reshape(M, OUT)
    bw = f64(base_w)[:, :HID, None]
    sw = f64(spline_w)[:, :HID] * f64(spline_scaler)[:, :HID, None]
    w2 = np.concatenate([bw, sw], axis=2).reshape(OUT, HID * (1 + COEF))
    da = (mxq(g, 1, "e5m2") @ mxq(w2, 0, "e4m3")).reshape(M, HID, 1 + COEF)
    sg = sigmoid(h)
    dh = da[..., 0] * (sg * (1.0 + h * (1.0 - sg))) + (da[..., 1:] * b_splines_grad(h, make_grid())).sum(2)
    dz1 = dh * (1.0 - h * h)
    dxf = mxq(dz1, 1, "e5m2") @ mxq(f64(Wx), 0, "e4m3")
    dwx = mxq(dz1, 0, "e5m2").T @ mxq(Xf, 0, "e4m3")
    return dxf.reshape(B, N, T_IN, FEAT).transpose(0, 2, 1, 3), dwx

@@ -1,0 +1,433 @@
+from contextlib import ExitStack
+import math
+
+import concourse.mybir as mybir
+from concourse.masks import make_identity
+
+F32 = mybir.dt.float32
+BF16 = mybir.dt.bfloat16
+U32 = mybir.dt.uint32
+U8 = mybir.dt.uint8
+E4 = mybir.dt.float8_e4m3fn_x4
+E5 = mybir.dt.float8_e5m2_x4
+ALU = mybir.AluOpType
+ACT = mybir.ActivationFunctionType
+
+FLOPS = 2 * 1024 * 512 * 4608 + 2 * 2 * 1024 * 512 * 1024
+BYTES = 2 * (1048576 + 524288 + 262144 + 2097152 + 262144 + 524288) + 4 * (524288 + 1048576 + 524288)
+
+P = 128
+PLUS, MINUS, PLUS4, MINUS4 = 0, 1, 2, 3
+VARIANT = (1.0, -1.0, 4.0, -4.0)
+TERMS = (
+    ("S", 0.4, ((0, PLUS),)),
+    ("OA", -0.5, ((5, PLUS), (3, MINUS))),
+    ("OB", -0.5, ((4, PLUS), (6, MINUS))),
+    ("L2", 0.5, ((2, PLUS), (6, MINUS))),
+    ("L1", 0.5, ((1, PLUS), (5, MINUS), (2, MINUS4), (6, PLUS4))),
+    ("R3", -0.5, ((7, PLUS), (3, MINUS))),
+    ("R4", -0.5, ((8, PLUS), (4, MINUS), (7, MINUS4), (3, PLUS4))),
+    ("F", -1.0, ((5, PLUS), (3, PLUS), (6, MINUS), (4, MINUS))),
+)
+ORDER = ((0, 0), (0, 1), (1, 0), (2, 0), (1, 1), (3, 0), (2, 1), (3, 1))
+
+
+def tile_refiner_pa_v_kernel(tc, X, Y, Wx, bx, Wy, by, base_w, spline_w, spline_scaler, Hx, grad_out, out_0, out_1):
+    nc = tc.nc
+    V, S, G, T = nc.vector, nc.scalar, nc.gpsimd, nc.tensor
+    with ExitStack() as ctx:
+        keep = ctx.enter_context(tc.tile_pool(name="keep", bufs=1))
+        work = ctx.enter_context(tc.tile_pool(name="work", bufs=1))
+        psum = ctx.enter_context(tc.psum_pool(name="psum", bufs=1))
+        ctx.enter_context(tc.manual_schedule())
+
+        def kt(shape, dt, name):
+            return keep.tile(shape, dt, name=name, tag=name, align_bytes=64)
+
+        def wt(shape, dt, tag, bufs):
+            return work.tile(shape, dt, name=tag, tag=tag, bufs=bufs, align_bytes=64)
+
+        def bank(tag, bufs):
+            return psum.tile([P, 512], F32, name=tag, tag=tag, bufs=bufs)
+
+        def stage():
+            return wt([P, 4096], BF16, "stage", 4)
+
+        def grp():
+            return wt([P, 2048], BF16, "grp", 4)
+
+        ident = kt([P, P], F32, "ident")
+        warm = kt([P, 1], F32, "warm")
+        V.memset(warm[:], 0.0)
+        S.activation(warm[:], warm[:], ACT.Sigmoid)
+        make_identity(nc, ident[:])
+
+        g_raw = stage()
+
+        def load_g(b):
+            nc.sync.dma_start(out=g_raw[:, b * 2048:(b + 1) * 2048].rearrange("p (j o) -> p j o", j=4),
+                              in_=grad_out[b].rearrange("(p j) o -> p j o", j=4))
+
+        hx = [kt([P, 4, 512], F32, "hx%d" % b) for b in range(2)]
+        sc = kt([P, 4, 512], BF16, "sc")
+        base = kt([P, 4, 512], BF16, "base")
+
+        def load_hx(b):
+            nc.sync.dma_start(out=hx[b][:], in_=Hx[b * 512:(b + 1) * 512, :].rearrange("(p j) i -> p j i", j=4))
+
+        def load_sp(it):
+            t = stage()
+            nc.sync.dma_start(out=t[:].rearrange("p (j w) -> p j w", j=4),
+                              in_=spline_w[:, it * P:(it + 1) * P, :].rearrange("(p j) i k -> p j (i k)", j=4))
+            return t
+
+        def load_x(b):
+            t = stage()
+            nc.sync.dma_start(out=t[:], in_=X[b].rearrange("t n f -> t (n f)"))
+            return t
+
+        sp = {}
+        load_g(0)
+        load_hx(0)
+        nc.sync.dma_start(out=sc[:], in_=spline_scaler[:, 0:512].rearrange("(p j) i -> p j i", j=4))
+        sp[0] = load_sp(0)
+        nc.sync.dma_start(out=base[:], in_=base_w[:, 0:512].rearrange("(p j) i -> p j i", j=4))
+        load_g(1)
+        load_hx(1)
+        sp[1] = load_sp(1)
+        sp[2] = load_sp(2)
+
+        gq = [kt([P, 1024], U32, "gq%d" % v) for v in range(4)]
+        gs = [kt([P, 1024], U8, "gs%d" % v) for v in range(4)]
+        bq = kt([P, 512], U32, "bq")
+        bs = kt([P, 512], U8, "bs")
+        wq = [kt([P, 1024], U32, "wq%d" % it) for it in range(4)]
+        ws = [kt([P, 1024], U8, "ws%d" % it) for it in range(4)]
+        dq = [kt([P, 512], U32, "dq%d" % b) for b in range(2)]
+        ds = [kt([P, 512], U8, "ds%d" % b) for b in range(2)]
+        eq = [kt([P, 512], U32, "eq%d" % b) for b in range(2)]
+        es = [kt([P, 512], U8, "es%d" % b) for b in range(2)]
+        xq = [kt([P, 1024], U32, "xq%d" % b) for b in range(2)]
+        xs = [kt([P, 1024], U8, "xs%d" % b) for b in range(2)]
+        vq = kt([P, 1024], U32, "vq")
+        vs = kt([P, 1024], U8, "vs")
+        dz = [kt([P, 512, 4], BF16, "dz%d" % b) for b in range(2)]
+
+        def g_transposes(b):
+            words = g_raw[:].bitcast(F32)
+            gg = grp()
+            ggw = gg[:].bitcast(F32)
+            for h in range(2):
+                pt = bank("misc", 2)
+                for jj in range(2):
+                    for u in range(2):
+                        w0 = (b * 4 + 2 * h + jj) * 256
+                        T.transpose(pt[:, (2 * jj + u) * P:(2 * jj + u + 1) * P], words[:, w0 + u:w0 + 256:2], ident[:])
+                S.copy(out=ggw[:, h * 512:(h + 1) * 512].rearrange("c (j p u) -> c j p u", j=2, u=2),
+                       in_=pt[:].rearrange("c (j u p) -> c j p u", j=2, u=2))
+            return gg
+
+        def g_variants(b, gg):
+            cols = slice(b * 512, (b + 1) * 512)
+            tiles = [gg]
+            for v in (1, 2, 3):
+                gv = grp()
+                V.tensor_scalar(out=gv[:], in0=gg[:], scalar1=VARIANT[v], scalar2=None, op0=ALU.mult)
+                tiles.append(gv)
+            for v in range(4):
+                V.quantize_mx(out=gq[v][:, cols].bitcast(E5), scales=gs[v][:, cols], in_=tiles[v][:])
+
+        def w2_base():
+            t = grp()
+            V.tensor_copy(out=t[:].rearrange("p (w j) -> p w j", j=4), in_=base[:].rearrange("p j w -> p w j"))
+            V.quantize_mx(out=bq[:].bitcast(E4), scales=bs[:], in_=t[:])
+
+        def w2_pieces(it):
+            raw = sp[it][:].rearrange("p (j q k) -> p k q j", j=4, k=8)
+            fac = sc[:, :, it * P:(it + 1) * P].rearrange("p j q -> p q j")
+            tiles = {}
+
+            def product(h, half):
+                def run():
+                    if half == 0:
+                        tiles[h] = grp()
+                    k0 = 4 * h + 2 * half
+                    V.tensor_tensor(out=tiles[h][:, half * 1024:(half + 1) * 1024].rearrange("p (k q j) -> p k q j", k=2, j=4),
+                                    in0=raw[:, k0:k0 + 2], in1=fac.unsqueeze(1).to_broadcast([P, 2, P, 4]), op=ALU.mult)
+                return run
+
+            def quant(h):
+                def run():
+                    cols = slice(h * 512, (h + 1) * 512)
+                    V.quantize_mx(out=wq[it][:, cols].bitcast(E4), scales=ws[it][:, cols], in_=tiles[h][:])
+                return run
+            return [product(0, 0), product(0, 1), product(1, 0), quant(0), product(1, 1), quant(1)]
+
+        ht = {}
+
+        def hx_transposes(n):
+            it, b = ORDER[n]
+            pt = bank("misc", 2)
+            for j in range(4):
+                T.transpose(pt[:, j * P:(j + 1) * P], hx[b][:, j, it * P:(it + 1) * P], ident[:])
+            ht[n] = wt([P, 512], F32, "ht", 2)
+            S.copy(out=ht[n][:], in_=pt[:])
+
+        wgt = {}
+        tmp = {}
+
+        def weights_scalar(n):
+            it, b = ORDER[n]
+            h = ht[n]
+            w = {name: wt([P, 512], F32, "w" + name, 2) for name in ("S", "OA", "OB", "L2", "L1", "R3", "R4", "F")}
+            a = wt([P, 512], F32, "ta", 1)
+            c = wt([P, 512], F32, "tb", 1)
+            q = wt([P, 512], F32, "tq", 1)
+            sg = wt([P, 512], F32, "sg", 1)
+            for name, op, knot in (("L1", ALU.min, -0.6), ("R4", ALU.max, 0.6)):
+                G.tensor_scalar(out=w[name][:], in0=h[:], scalar1=knot, scalar2=-knot, op0=op, op1=ALU.add)
+            S.activation(a[:], h[:], ACT.Abs, bias=0.5, scale=2.5)
+            S.activation(c[:], h[:], ACT.Abs, bias=-0.5, scale=2.5)
+            S.activation(sg[:], h[:], ACT.Sigmoid)
+            S.activation(a[:], a[:], ACT.Abs, bias=-2.0)
+            S.activation(c[:], c[:], ACT.Abs, bias=-2.0)
+            S.activation(q[:], a[:], ACT.Abs, bias=-1.0)
+            S.activation(w["L2"][:], h[:], ACT.Relu, bias=-0.5, scale=-2.5)
+            S.activation(w["L2"][:], w["L2"][:], ACT.Square)
+            S.activation(w["R3"][:], h[:], ACT.Relu, bias=-0.5, scale=2.5)
+            S.activation(w["L1"][:], w["L1"][:], ACT.Square, scale=2.5)
+            S.activation(w["R3"][:], w["R3"][:], ACT.Square)
+            S.activation(w["R4"][:], w["R4"][:], ACT.Square, scale=2.5)
+            wgt[n] = w
+            tmp[n] = (a, c, q, sg)
+
+        sqs = {}
+
+        def square(n):
+            it, b = ORDER[n]
+            sqs[n] = wt([P, 4, P], F32, "sq", 2)
+            S.activation(sqs[n][:], hx[b][:, :, it * P:(it + 1) * P], ACT.Square, scale=math.sqrt(2.5))
+
+        def weights_vector(n):
+            w = wgt[n]
+            a, c, q, sg = tmp[n]
+            h = ht[n]
+
+            def one():
+                V.tensor_scalar(out=a[:], in0=a[:], scalar1=-1.0, scalar2=1.0, op0=ALU.mult, op1=ALU.add)
+                V.tensor_scalar(out=c[:], in0=c[:], scalar1=-1.0, scalar2=1.0, op0=ALU.mult, op1=ALU.add)
+
+            def two():
+                V.scalar_tensor_tensor(out=w["S"][:], in0=sg[:], scalar=1.0, in1=h[:], op0=ALU.subtract, op1=ALU.mult)
+                V.scalar_tensor_tensor(out=w["OA"][:], in0=q[:], scalar=2.0, in1=a[:], op0=ALU.subtract, op1=ALU.mult)
+                G.tensor_tensor(out=w["F"][:], in0=a[:], in1=c[:], op=ALU.mult)
+
+            def three():
+                V.scalar_tensor_tensor(out=w["S"][:], in0=w["S"][:], scalar=1.0, in1=sg[:], op0=ALU.subtract, op1=ALU.mult)
+                V.scalar_tensor_tensor(out=w["OB"][:], in0=q[:], scalar=1.0, in1=c[:], op0=ALU.add, op1=ALU.mult)
+            return [one, two, three]
+
+        prod = {}
+
+        def term_passes(n, r):
+            it, b = ORDER[n]
+            name, const, passes = TERMS[r]
+            da = bank("da", 4)
+            cols = slice(b * 512, (b + 1) * 512)
+            for s, (c, v) in enumerate(passes):
+                if c == 0:
+                    lq, ls = bq[:, it * P:(it + 1) * P], bs[:, it * P:(it + 1) * P]
+                else:
+                    lq, ls = wq[it][:, (c - 1) * P:c * P], ws[it][:, (c - 1) * P:c * P]
+                T.matmul_mx(out=da[:], lhsT=lq.bitcast(E4), lhsT_scale=ls, rhs=gq[v][:, cols].bitcast(E5), rhs_scale=gs[v][:, cols],
+                            start=(s == 0), stop=(s == len(passes) - 1))
+            pr = wt([P, 512], F32, "prod", 12)
+            V.scalar_tensor_tensor(out=pr[:], in0=wgt[n][name][:], scalar=const, in1=da[:], op0=ALU.mult, op1=ALU.mult)
+            prod[n, r] = pr
+
+        sums = {}
+
+        def sum_transposes(n):
+            sm = bank("sum", 2)
+            for j in range(4):
+                js = slice(j * P, (j + 1) * P)
+                for r in range(len(TERMS)):
+                    T.matmul(sm[:, js], lhsT=prod[n, r][:, js], rhs=ident[:], is_transpose=True, start=(r == 0), stop=(r == len(TERMS) - 1))
+            sums[n] = sm
+
+        def dz_final(n):
+            it, b = ORDER[n]
+            sq = sqs[n]
+            V.scalar_tensor_tensor(out=dz[b][:, it * P:(it + 1) * P, :], in0=sq[:].rearrange("p j q -> p q j"), scalar=2.5,
+                                   in1=sums[n][:].rearrange("p (j q) -> p q j", j=4), op0=ALU.subtract, op1=ALU.mult)
+
+        def dz_quant(n):
+            it, b = ORDER[n]
+            isl = slice(it * P, (it + 1) * P)
+            V.quantize_mx(out=dq[b][:, isl].bitcast(E5), scales=ds[b][:, isl], in_=dz[b][:, isl, :].rearrange("p q j -> p (q j)"))
+
+        def dz2(b, copies):
+            words = dz[b][:].rearrange("p i j -> p (i j)").bitcast(F32)
+            t2 = grp()
+            for v in range(2):
+                pt = bank("misc", 2)
+                for t in range(4):
+                    T.transpose(pt[:, t * P:(t + 1) * P], words[:, 2 * t + v::8], ident[:])
+                dst = t2[:, v * 1024:(v + 1) * 1024].rearrange("c (e p t) -> c e p t", e=2, t=4)
+                src = pt[:].bitcast(BF16).rearrange("c (t p e) -> c e p t", t=4, e=2)
+                if copies[v] == "v":
+                    V.tensor_copy(out=dst, in_=src)
+                else:
+                    S.copy(out=dst, in_=src)
+            return t2
+
+        def dz2_quant(b, t2):
+            V.quantize_mx(out=eq[b][:].bitcast(E5), scales=es[b][:], in_=t2[:])
+
+        def wx_prep():
+            raw = stage()
+            nc.sync.dma_start(out=raw[:].rearrange("p (j w) -> p j w", j=4), in_=Wx.rearrange("(p j) w -> p j w", j=4))
+            rv = raw[:].rearrange("p (j w) -> p w j", j=4)
+            tiles = [grp(), grp()]
+
+            def cp(h):
+                def run():
+                    V.tensor_copy(out=tiles[h][:].rearrange("p (w j) -> p w j", j=4), in_=rv[:, h * 512:(h + 1) * 512, :])
+                return run
+
+            def qn(h):
+                def run():
+                    V.quantize_mx(out=vq[:, h * 512:(h + 1) * 512].bitcast(E4), scales=vs[:, h * 512:(h + 1) * 512], in_=tiles[h][:])
+                return run
+            return [cp(0), cp(1), qn(0), qn(1)]
+
+        xg = {}
+
+        def x_bank(b, xt, w):
+            if w == 0:
+                xg[b] = wt([P, 4096], BF16, "ot", 2)
+            words = xt[:].bitcast(F32)
+            pt = bank("misc", 2)
+            for j in range(4):
+                T.transpose(pt[:, j * P:(j + 1) * P], words[:, 4 * j + w::16], ident[:])
+            S.copy(out=xg[b][:].rearrange("p (t f j) -> p t f j", f=8, j=4)[:, :, 2 * w:2 * w + 2, :],
+                   in_=pt[:].bitcast(BF16).rearrange("p (j t e) -> p t e j", j=4, e=2))
+
+        def x_quant(b):
+            V.quantize_mx(out=xq[b][:].bitcast(E4), scales=xs[b][:], in_=xg[b][:])
+
+        def out1(it, engines):
+            o = wt([P, 2048], F32, "ot", 2)
+            for h in range(2):
+                pt = bank("misc", 2)
+                for b in range(2):
+                    T.matmul_mx(out=pt[:], lhsT=dq[b][:, it * P:(it + 1) * P].bitcast(E5), lhsT_scale=ds[b][:, it * P:(it + 1) * P],
+                                rhs=xq[b][:, h * 512:(h + 1) * 512].bitcast(E4), rhs_scale=xs[b][:, h * 512:(h + 1) * 512],
+                                start=(b == 0), stop=(b == 1))
+                if engines[h] == "v":
+                    V.tensor_copy(out=o[:, h * 512:(h + 1) * 512], in_=pt[:])
+                else:
+                    S.copy(out=o[:, h * 512:(h + 1) * 512], in_=pt[:])
+            nc.sync.dma_start(out=out_1[it * P:(it + 1) * P, :], in_=o[:, 0:1024])
+
+        def out0(b, h, engines):
+            o = wt([P, 2048], F32, "ot", 2)
+            ov = o[:].rearrange("p (t j f) -> p t j f", j=4, f=8)
+            for j in range(4):
+                pt = bank("misc", 2)
+                T.matmul_mx(out=pt[:], lhsT=eq[b][:, j * P:(j + 1) * P].bitcast(E5), lhsT_scale=es[b][:, j * P:(j + 1) * P],
+                            rhs=vq[:, h * 512:(h + 1) * 512].bitcast(E4), rhs_scale=vs[:, h * 512:(h + 1) * 512], start=True, stop=True)
+                src = pt[:].rearrange("p (t f) -> p t f", f=8)
+                if engines[j] == "v":
+                    V.tensor_copy(out=ov[:, :, j, :], in_=src)
+                else:
+                    S.copy(out=ov[:, :, j, :], in_=src)
+            nc.sync.dma_start(out=out_0[b, h * 64:(h + 1) * 64].rearrange("t (p j) f -> p t (j f)", j=4),
+                              in_=o[:].rearrange("p (t r) -> p t r", r=32))
+
+        gg0 = g_transposes(0)
+        hx_transposes(0)
+        weights_scalar(0)
+        g_variants(0, gg0)
+        pieces = w2_pieces(0)
+        for step in pieces[:3]:
+            step()
+        for step in weights_vector(0):
+            step()
+        for step in pieces[3:]:
+            step()
+        w2_base()
+        gg1 = g_transposes(1)
+        hx_transposes(1)
+
+        xt = {}
+
+        def slot(n, tasks):
+            for r in range(len(TERMS)):
+                term_passes(n, r)
+                for task in tasks.get(r, ()):
+                    task()
+                if r == 3:
+                    if n > 0:
+                        sum_transposes(n - 1)
+                    if n + 2 < len(ORDER):
+                        hx_transposes(n + 2)
+                if n > 0 and r == 4:
+                    dz_final(n - 1)
+                if r == 4:
+                    square(n)
+                if n > 0 and r == 5:
+                    dz_quant(n - 1)
+
+        def spread(steps, first):
+            d = {}
+            for k, s in enumerate(steps):
+                d.setdefault(min(first + k, 7), []).append(s)
+            return d
+
+        def merge(*maps):
+            d = {}
+            for m in maps:
+                for k, v in m.items():
+                    d.setdefault(k, []).extend(v)
+            return d
+
+        for n in range(len(ORDER)):
+            it, b = ORDER[n]
+            if n + 1 < len(ORDER):
+                weights_scalar(n + 1)
+                wv = spread(weights_vector(n + 1), 5)
+            else:
+                wv = {}
+            extra = {}
+            if n == 0:
+                extra = {1: [lambda: g_variants(1, gg1)]}
+            elif n == 1:
+                extra = spread(w2_pieces(1), 0)
+                steps = wx_prep()
+                xt[0] = load_x(0)
+            elif n == 2:
+                extra = spread(w2_pieces(2), 0)
+                sp[3] = load_sp(3)
+            elif n == 3:
+                extra = merge(spread(steps, 0), {3: [lambda: x_bank(0, xt[0], 0), lambda: x_bank(0, xt[0], 1), lambda: x_bank(0, xt[0], 2), lambda: x_bank(0, xt[0], 3)]})
+                xt[1] = load_x(1)
+            elif n == 4:
+                extra = merge(spread(w2_pieces(3), 0), {7: [lambda: x_quant(0)]})
+            elif n == 5:
+                extra = {3: [lambda: x_bank(1, xt[1], 0), lambda: x_bank(1, xt[1], 1), lambda: x_bank(1, xt[1], 2), lambda: x_bank(1, xt[1], 3)], 7: [lambda: x_quant(1)]}
+            elif n == 6:
+                extra = {1: [lambda: out1(0, "ss")], 6: [lambda: tmp.setdefault("t2", dz2(0, "ss"))], 7: [lambda: dz2_quant(0, tmp["t2"]), lambda: out1(1, "ss")]}
+            elif n == 7:
+                extra = {1: [lambda: out0(0, 0, "ssss")], 6: [lambda: out0(0, 1, "ssss")]}
+            slot(n, merge(extra, wv))
+
+        sum_transposes(7)
+        dz_final(7)
+        t2 = dz2(1, "vs")
+        dz2_quant(1, t2)
+        dz_quant(7)
+        out0(1, 0, "vsvs")
+        out1(2, "vs")
+        out0(1, 1, "vsvs")
+        out1(3, "vs")

@@ -11,23 +11,37 @@ U8 = mybir.dt.uint8
 E4 = mybir.dt.float8_e4m3fn_x4
 E5 = mybir.dt.float8_e5m2_x4
 ALU = mybir.AluOpType
+OPS = {"mult": ALU.mult, "min": ALU.min, "max": ALU.max}
 ACT = mybir.ActivationFunctionType
 
 FLOPS = 2 * 1024 * 512 * 4608 + 2 * 2 * 1024 * 512 * 1024
 BYTES = 2 * (1048576 + 524288 + 262144 + 2097152 + 262144 + 524288) + 4 * (524288 + 1048576 + 524288)
 
 P = 128
-PLUS, MINUS, PLUS4, MINUS4 = 0, 1, 2, 3
-VARIANT = (1.0, -1.0, 4.0, -4.0)
+SUM_AT = 4
+NEG, POS4, NEG4, NEG2 = 0, 1, 2, 3
+VARIANT = (-1.0, 4.0, -4.0, -2.0)
+CHAIN = ((NEG,), (POS4,), (NEG4, NEG2), (POS4,))
+
+
+def left(j):
+    return tuple((1 + k, v) for k in range(j - 1, 4) for v in CHAIN[k + 1 - j])
+
+
+def right(j):
+    return tuple((1 + k, v) for k in range(7, 3, -1) if 0 <= j - (k - 3) for v in CHAIN[j - (k - 3)])
+
+
 TERMS = (
-    ("S", 0.4, ((0, PLUS),)),
-    ("OA", -0.5, ((5, PLUS), (3, MINUS))),
-    ("OB", -0.5, ((4, PLUS), (6, MINUS))),
-    ("L2", 0.5, ((2, PLUS), (6, MINUS))),
-    ("L1", 0.5, ((1, PLUS), (5, MINUS), (2, MINUS4), (6, PLUS4))),
-    ("R3", -0.5, ((7, PLUS), (3, MINUS))),
-    ("R4", -0.5, ((8, PLUS), (4, MINUS), (7, MINUS4), (3, PLUS4))),
-    ("F", -1.0, ((5, PLUS), (3, PLUS), (6, MINUS), (4, MINUS))),
+    ("S", "mult", -0.8, ((0, NEG),)),
+    ("L2", "mult", -1.0, left(2)),
+    ("R2", "mult", 1.0, right(2)),
+    ("s3", "min", 0.0, left(3)),
+    ("s3", "max", 0.0, right(3)),
+    ("L1", "mult", -1.0, left(1)),
+    ("R1", "mult", 1.0, right(1)),
+    ("L4", "mult", -1.0, left(4)),
+    ("R4", "mult", 1.0, right(4)),
 )
 ORDER = ((0, 0), (0, 1), (1, 0), (2, 0), (1, 1), (3, 0), (2, 1), (3, 1))
 
@@ -115,7 +129,7 @@ def tile_refiner_pa_v_kernel(tc, X, Y, Wx, bx, Wy, by, base_w, spline_w, spline_
 
         def g_transposes(b):
             words = g_raw[:].bitcast(F32)
-            gg = grp()
+            gg = wt([P, 2048], BF16, "gg", 1)
             ggw = gg[:].bitcast(F32)
             for h in range(2):
                 pt = bank("misc", 2)
@@ -127,19 +141,29 @@ def tile_refiner_pa_v_kernel(tc, X, Y, Wx, bx, Wy, by, base_w, spline_w, spline_
                        in_=pt[:].rearrange("c (j u p) -> c j p u", j=2, u=2))
             return gg
 
-        def g_variants(b, gg):
+        def g_variants_steps(b, gg):
             cols = slice(b * 512, (b + 1) * 512)
-            tiles = [gg]
-            for v in (1, 2, 3):
-                gv = grp()
-                V.tensor_scalar(out=gv[:], in0=gg[:], scalar1=VARIANT[v], scalar2=None, op0=ALU.mult)
-                tiles.append(gv)
-            for v in range(4):
-                V.quantize_mx(out=gq[v][:, cols].bitcast(E5), scales=gs[v][:, cols], in_=tiles[v][:])
+            tiles = {}
+
+            def scaled(v):
+                def run():
+                    tiles[v] = grp()
+                    V.tensor_scalar(out=tiles[v][:], in0=gg[:], scalar1=VARIANT[v], scalar2=None, op0=ALU.mult)
+                return run
+
+            def quant(v):
+                def run():
+                    V.quantize_mx(out=gq[v][:, cols].bitcast(E5), scales=gs[v][:, cols], in_=tiles[v][:])
+                return run
+            return [scaled(0), scaled(1), quant(0), scaled(2), quant(1), scaled(3), quant(2), quant(3)]
+
+        def g_variants(b, gg):
+            for step in g_variants_steps(b, gg):
+                step()
 
         def w2_base():
             t = grp()
-            V.tensor_copy(out=t[:].rearrange("p (w j) -> p w j", j=4), in_=base[:].rearrange("p j w -> p w j"))
+            S.copy(out=t[:].rearrange("p (w j) -> p w j", j=4), in_=base[:].rearrange("p j w -> p w j"))
             V.quantize_mx(out=bq[:].bitcast(E4), scales=bs[:], in_=t[:])
 
         def w2_pieces(it):
@@ -176,62 +200,63 @@ def tile_refiner_pa_v_kernel(tc, X, Y, Wx, bx, Wy, by, base_w, spline_w, spline_
         wgt = {}
         tmp = {}
 
-        def weights_scalar(n):
-            it, b = ORDER[n]
+        def weights(n):
             h = ht[n]
-            w = {name: wt([P, 512], F32, "w" + name, 2) for name in ("S", "OA", "OB", "L2", "L1", "R3", "R4", "F")}
-            a = wt([P, 512], F32, "ta", 1)
-            c = wt([P, 512], F32, "tb", 1)
-            q = wt([P, 512], F32, "tq", 1)
-            sg = wt([P, 512], F32, "sg", 1)
-            for name, op, knot in (("L1", ALU.min, -0.6), ("R4", ALU.max, 0.6)):
-                G.tensor_scalar(out=w[name][:], in0=h[:], scalar1=knot, scalar2=-knot, op0=op, op1=ALU.add)
-            S.activation(a[:], h[:], ACT.Abs, bias=0.5, scale=2.5)
-            S.activation(c[:], h[:], ACT.Abs, bias=-0.5, scale=2.5)
-            S.activation(sg[:], h[:], ACT.Sigmoid)
-            S.activation(a[:], a[:], ACT.Abs, bias=-2.0)
-            S.activation(c[:], c[:], ACT.Abs, bias=-2.0)
-            S.activation(q[:], a[:], ACT.Abs, bias=-1.0)
-            S.activation(w["L2"][:], h[:], ACT.Relu, bias=-0.5, scale=-2.5)
-            S.activation(w["L2"][:], w["L2"][:], ACT.Square)
-            S.activation(w["R3"][:], h[:], ACT.Relu, bias=-0.5, scale=2.5)
-            S.activation(w["L1"][:], w["L1"][:], ACT.Square, scale=2.5)
-            S.activation(w["R3"][:], w["R3"][:], ACT.Square)
-            S.activation(w["R4"][:], w["R4"][:], ACT.Square, scale=2.5)
+            w = {}
+            steps = {}
+
+            def sigmoid():
+                tmp[n] = wt([P, 512], F32, "sg", 1)
+                S.activation(tmp[n][:], h[:], ACT.Sigmoid)
+
+            def silu_a():
+                w["S"] = wt([P, 512], F32, "wS", 2)
+                V.scalar_tensor_tensor(out=w["S"][:], in0=tmp[n][:], scalar=1.0, in1=h[:], op0=ALU.subtract, op1=ALU.mult)
+
+            def silu_b():
+                V.scalar_tensor_tensor(out=w["S"][:], in0=w["S"][:], scalar=1.0, in1=tmp[n][:], op0=ALU.subtract, op1=ALU.mult)
+
+            def dist(j):
+                def run():
+                    w["s%d" % j] = wt([P, 512], F32, "ws%d" % j, 2)
+                    S.activation(w["s%d" % j][:], h[:], ACT.Abs, bias=6.25 - 2.5 * j, scale=6.25)
+                return run
+
+            def signed(j):
+                def run():
+                    t = w["s%d" % j]
+                    V.scalar_tensor_tensor(out=t[:], in0=h[:], scalar=0.4 * j - 1.0, in1=t[:], op0=ALU.subtract, op1=ALU.mult)
+                return run
+
+            def relu(side, j):
+                def run():
+                    t = wt([P, 512], F32, "w%s%d" % (side, j), 2)
+                    w["%s%d" % (side, j)] = t
+                    sign = 1.0 if side == "R" else -1.0
+                    S.activation(t[:], h[:], ACT.Relu, bias=sign * (2.5 - j), scale=sign * 2.5)
+                return run
+
+            def square_(side, j):
+                def run():
+                    t = w["%s%d" % (side, j)]
+                    S.activation(t[:], t[:], ACT.Square)
+                return run
             wgt[n] = w
-            tmp[n] = (a, c, q, sg)
+            return {0: [sigmoid, relu("L", 2)], 1: [dist(3), square_("L", 2), relu("R", 2)], 2: [silu_a, square_("R", 2), relu("L", 1)], 3: [signed(3), square_("L", 1), relu("R", 1)],
+                    4: [silu_b, square_("R", 1), relu("L", 4)], 5: [square_("L", 4)], 6: [relu("R", 4)], 7: [square_("R", 4)]}
 
         sqs = {}
 
         def square(n):
             it, b = ORDER[n]
             sqs[n] = wt([P, 4, P], F32, "sq", 2)
-            S.activation(sqs[n][:], hx[b][:, :, it * P:(it + 1) * P], ACT.Square, scale=math.sqrt(2.5))
-
-        def weights_vector(n):
-            w = wgt[n]
-            a, c, q, sg = tmp[n]
-            h = ht[n]
-
-            def one():
-                V.tensor_scalar(out=a[:], in0=a[:], scalar1=-1.0, scalar2=1.0, op0=ALU.mult, op1=ALU.add)
-                V.tensor_scalar(out=c[:], in0=c[:], scalar1=-1.0, scalar2=1.0, op0=ALU.mult, op1=ALU.add)
-
-            def two():
-                V.scalar_tensor_tensor(out=w["S"][:], in0=sg[:], scalar=1.0, in1=h[:], op0=ALU.subtract, op1=ALU.mult)
-                V.scalar_tensor_tensor(out=w["OA"][:], in0=q[:], scalar=2.0, in1=a[:], op0=ALU.subtract, op1=ALU.mult)
-                G.tensor_tensor(out=w["F"][:], in0=a[:], in1=c[:], op=ALU.mult)
-
-            def three():
-                V.scalar_tensor_tensor(out=w["S"][:], in0=w["S"][:], scalar=1.0, in1=sg[:], op0=ALU.subtract, op1=ALU.mult)
-                V.scalar_tensor_tensor(out=w["OB"][:], in0=q[:], scalar=1.0, in1=c[:], op0=ALU.add, op1=ALU.mult)
-            return [one, two, three]
+            S.activation(sqs[n][:], hx[b][:, :, it * P:(it + 1) * P], ACT.Square, scale=math.sqrt(1.25))
 
         prod = {}
 
         def term_passes(n, r):
             it, b = ORDER[n]
-            name, const, passes = TERMS[r]
+            name, op, const, passes = TERMS[r]
             da = bank("da", 4)
             cols = slice(b * 512, (b + 1) * 512)
             for s, (c, v) in enumerate(passes):
@@ -241,8 +266,8 @@ def tile_refiner_pa_v_kernel(tc, X, Y, Wx, bx, Wy, by, base_w, spline_w, spline_
                     lq, ls = wq[it][:, (c - 1) * P:c * P], ws[it][:, (c - 1) * P:c * P]
                 T.matmul_mx(out=da[:], lhsT=lq.bitcast(E4), lhsT_scale=ls, rhs=gq[v][:, cols].bitcast(E5), rhs_scale=gs[v][:, cols],
                             start=(s == 0), stop=(s == len(passes) - 1))
-            pr = wt([P, 512], F32, "prod", 12)
-            V.scalar_tensor_tensor(out=pr[:], in0=wgt[n][name][:], scalar=const, in1=da[:], op0=ALU.mult, op1=ALU.mult)
+            pr = wt([P, 512], F32, "prod", 14)
+            V.scalar_tensor_tensor(out=pr[:], in0=wgt[n][name][:], scalar=const, in1=da[:], op0=OPS[op], op1=ALU.mult)
             prod[n, r] = pr
 
         sums = {}
@@ -258,7 +283,7 @@ def tile_refiner_pa_v_kernel(tc, X, Y, Wx, bx, Wy, by, base_w, spline_w, spline_
         def dz_final(n):
             it, b = ORDER[n]
             sq = sqs[n]
-            V.scalar_tensor_tensor(out=dz[b][:, it * P:(it + 1) * P, :], in0=sq[:].rearrange("p j q -> p q j"), scalar=2.5,
+            V.scalar_tensor_tensor(out=dz[b][:, it * P:(it + 1) * P, :], in0=sq[:].rearrange("p j q -> p q j"), scalar=1.25,
                                    in1=sums[n][:].rearrange("p (j q) -> p q j", j=4), op0=ALU.subtract, op1=ALU.mult)
 
         def dz_quant(n):
@@ -292,7 +317,7 @@ def tile_refiner_pa_v_kernel(tc, X, Y, Wx, bx, Wy, by, base_w, spline_w, spline_
 
             def cp(h):
                 def run():
-                    V.tensor_copy(out=tiles[h][:].rearrange("p (w j) -> p w j", j=4), in_=rv[:, h * 512:(h + 1) * 512, :])
+                    S.copy(out=tiles[h][:].rearrange("p (w j) -> p w j", j=4), in_=rv[:, h * 512:(h + 1) * 512, :])
                 return run
 
             def qn(h):
@@ -316,8 +341,11 @@ def tile_refiner_pa_v_kernel(tc, X, Y, Wx, bx, Wy, by, base_w, spline_w, spline_
         def x_quant(b):
             V.quantize_mx(out=xq[b][:].bitcast(E4), scales=xs[b][:], in_=xg[b][:])
 
-        def out1(it, engines):
-            o = wt([P, 2048], F32, "ot", 2)
+        def out_tile(tail):
+            return stage()[:].bitcast(F32) if tail else wt([P, 2048], F32, "ot", 2)[:]
+
+        def out1(it, engines, tail=False):
+            o = out_tile(tail)
             for h in range(2):
                 pt = bank("misc", 2)
                 for b in range(2):
@@ -330,9 +358,9 @@ def tile_refiner_pa_v_kernel(tc, X, Y, Wx, bx, Wy, by, base_w, spline_w, spline_
                     S.copy(out=o[:, h * 512:(h + 1) * 512], in_=pt[:])
             nc.sync.dma_start(out=out_1[it * P:(it + 1) * P, :], in_=o[:, 0:1024])
 
-        def out0(b, h, engines):
-            o = wt([P, 2048], F32, "ot", 2)
-            ov = o[:].rearrange("p (t j f) -> p t j f", j=4, f=8)
+        def out0(b, h, engines, tail=False):
+            o = out_tile(tail)
+            ov = o.rearrange("p (t j f) -> p t j f", j=4, f=8)
             for j in range(4):
                 pt = bank("misc", 2)
                 T.matmul_mx(out=pt[:], lhsT=eq[b][:, j * P:(j + 1) * P].bitcast(E5), lhsT_scale=es[b][:, j * P:(j + 1) * P],
@@ -343,47 +371,50 @@ def tile_refiner_pa_v_kernel(tc, X, Y, Wx, bx, Wy, by, base_w, spline_w, spline_
                 else:
                     S.copy(out=ov[:, :, j, :], in_=src)
             nc.sync.dma_start(out=out_0[b, h * 64:(h + 1) * 64].rearrange("t (p j) f -> p t (j f)", j=4),
-                              in_=o[:].rearrange("p (t r) -> p t r", r=32))
+                              in_=o.rearrange("p (t r) -> p t r", r=32))
 
         gg0 = g_transposes(0)
         hx_transposes(0)
-        weights_scalar(0)
+        first = weights(0)
+        for k in (0, 1):
+            for step in first[k]:
+                step()
         g_variants(0, gg0)
         pieces = w2_pieces(0)
-        for step in pieces[:3]:
-            step()
-        for step in weights_vector(0):
-            step()
+        w2_base()
+        pieces[0]()
+        for k in (2, 3):
+            for step in first[k]:
+                step()
+        pieces[1]()
+        pieces[2]()
+        for k in (4, 5, 6, 7):
+            for step in first[k]:
+                step()
         for step in pieces[3:]:
             step()
-        w2_base()
         gg1 = g_transposes(1)
         hx_transposes(1)
 
         xt = {}
+        t2 = {}
 
         def slot(n, tasks):
             for r in range(len(TERMS)):
                 term_passes(n, r)
                 for task in tasks.get(r, ()):
                     task()
-                if r == 3:
+                if r == SUM_AT:
                     if n > 0:
                         sum_transposes(n - 1)
                     if n + 2 < len(ORDER):
                         hx_transposes(n + 2)
-                if n > 0 and r == 4:
+                if n > 0 and r == SUM_AT + 1:
                     dz_final(n - 1)
-                if r == 4:
+                if r == SUM_AT + 1:
                     square(n)
-                if n > 0 and r == 5:
+                if n > 0 and r == SUM_AT + 2:
                     dz_quant(n - 1)
-
-        def spread(steps, first):
-            d = {}
-            for k, s in enumerate(steps):
-                d.setdefault(min(first + k, 7), []).append(s)
-            return d
 
         def merge(*maps):
             d = {}
@@ -392,42 +423,46 @@ def tile_refiner_pa_v_kernel(tc, X, Y, Wx, bx, Wy, by, base_w, spline_w, spline_
                     d.setdefault(k, []).extend(v)
             return d
 
+        def spread(steps, where):
+            d = {}
+            for k, s in zip(where, steps):
+                d.setdefault(k, []).append(s)
+            return d
+
+        def xb(b, w):
+            return lambda: x_bank(b, xt[b], w)
+
         for n in range(len(ORDER)):
-            it, b = ORDER[n]
-            if n + 1 < len(ORDER):
-                weights_scalar(n + 1)
-                wv = spread(weights_vector(n + 1), 5)
-            else:
-                wv = {}
+            nxt = weights(n + 1) if n + 1 < len(ORDER) else {}
             extra = {}
             if n == 0:
-                extra = {1: [lambda: g_variants(1, gg1)]}
+                extra = spread(g_variants_steps(1, gg1), (0, 1, 2, 3, 4, 5, 6, 7))
             elif n == 1:
-                extra = spread(w2_pieces(1), 0)
+                extra = spread(w2_pieces(1), (0, 1, 3, 5, 6, 7))
                 steps = wx_prep()
                 xt[0] = load_x(0)
             elif n == 2:
-                extra = spread(w2_pieces(2), 0)
+                extra = merge(spread(w2_pieces(2), (0, 1, 3, 5, 6, 7)), spread([xb(0, 0), xb(0, 1)], (2, 7)))
                 sp[3] = load_sp(3)
             elif n == 3:
-                extra = merge(spread(steps, 0), {3: [lambda: x_bank(0, xt[0], 0), lambda: x_bank(0, xt[0], 1), lambda: x_bank(0, xt[0], 2), lambda: x_bank(0, xt[0], 3)]})
+                extra = merge(spread(steps, (0, 2, 4, 6)), spread([xb(0, 2), xb(0, 3)], (1, 7)))
                 xt[1] = load_x(1)
             elif n == 4:
-                extra = merge(spread(w2_pieces(3), 0), {7: [lambda: x_quant(0)]})
+                extra = merge(spread(w2_pieces(3), (0, 1, 3, 5, 6, 7)), spread([xb(1, 0), xb(1, 1)], (2, 7)), {8: [lambda: x_quant(0)]})
             elif n == 5:
-                extra = {3: [lambda: x_bank(1, xt[1], 0), lambda: x_bank(1, xt[1], 1), lambda: x_bank(1, xt[1], 2), lambda: x_bank(1, xt[1], 3)], 7: [lambda: x_quant(1)]}
+                extra = merge(spread([xb(1, 2), xb(1, 3)], (1, 3)), {5: [lambda: x_quant(1)], 6: [lambda: out1(0, "ss")]})
             elif n == 6:
-                extra = {1: [lambda: out1(0, "ss")], 6: [lambda: tmp.setdefault("t2", dz2(0, "ss"))], 7: [lambda: dz2_quant(0, tmp["t2"]), lambda: out1(1, "ss")]}
+                extra = {6: [lambda: t2.setdefault(0, dz2(0, "ss"))], 7: [lambda: dz2_quant(0, t2[0])], 8: [lambda: out0(0, 0, "ssss")]}
             elif n == 7:
-                extra = {1: [lambda: out0(0, 0, "ssss")], 6: [lambda: out0(0, 1, "ssss")]}
-            slot(n, merge(extra, wv))
+                extra = {2: [lambda: out0(0, 1, "ssss")], 7: [lambda: out1(1, "ss")]}
+            slot(n, merge(extra, nxt))
 
         sum_transposes(7)
+        out1(2, "vs", True)
         dz_final(7)
-        t2 = dz2(1, "vs")
-        dz2_quant(1, t2)
+        t2[1] = dz2(1, "vs")
+        dz2_quant(1, t2[1])
         dz_quant(7)
-        out0(1, 0, "vsvs")
-        out1(2, "vs")
-        out0(1, 1, "vsvs")
-        out1(3, "vs")
+        out0(1, 0, "vsvs", True)
+        out0(1, 1, "vsvs", True)
+        out1(3, "vs", True)

@@ -11,8 +11,8 @@ U8 = mybir.dt.uint8
 E4 = mybir.dt.float8_e4m3fn_x4
 E5 = mybir.dt.float8_e5m2_x4
 ALU = mybir.AluOpType
-OPS = {"mult": ALU.mult, "min": ALU.min, "max": ALU.max}
 ACT = mybir.ActivationFunctionType
+OPS = {"sub": ALU.subtract, "mult": ALU.mult, "min": ALU.min, "max": ALU.max}
 
 FLOPS = 2 * 1024 * 512 * 4608 + 2 * 2 * 1024 * 512 * 1024
 BYTES = 2 * (1048576 + 524288 + 262144 + 2097152 + 262144 + 524288) + 4 * (524288 + 1048576 + 524288)
@@ -33,22 +33,38 @@ def right(j):
 
 
 TERMS = (
-    ("S", "mult", -0.8, ((0, NEG),)),
+    ("T", "sub", 1.0, ((0, NEG),)),
     ("L2", "mult", -1.0, left(2)),
     ("R2", "mult", 1.0, right(2)),
-    ("s3", "min", 0.0, left(3)),
-    ("s3", "max", 0.0, right(3)),
+    ("L3", "mult", -1.0, left(3)),
+    ("R3", "mult", 1.0, right(3)),
     ("L1", "mult", -1.0, left(1)),
     ("R1", "mult", 1.0, right(1)),
     ("L4", "mult", -1.0, left(4)),
     ("R4", "mult", 1.0, right(4)),
 )
+NT = len(TERMS)
+PRODS = 10
 ORDER = ((0, 0), (0, 1), (1, 0), (2, 0), (1, 1), (3, 0), (2, 1), (3, 1))
+PLAN = {
+    0: ((0, "gv1.0"), (0, "gv1.3"), (0, "gv1.2"), (1, "gv1.5"), (3, "gv1.1"), (3, "w1.0"), (4, "gv1.4"), (6, "w1.2"), (6, "gv1.7"), (6, "gv1.6"), (6, "base1")),
+    1: ((1, "w2.0"), (1, "w1.4"), (1, "w2.1"), (1, "w1.1"), (3, "base2"), (4, "w1.3"), (6, "base3"), (6, "w1.5"), (7, "w2.3")),
+    2: ((1, "w2.2"), (2, "w2.4"), (4, "w2.5"), (8, "w3.0")),
+    3: ((1, "x0.0"), (2, "w3.1"), (3, "w3.3")),
+    4: ((0, "w3.2"), (1, "w3.4"), (2, "x0.1"), (7, "w3.5")),
+    5: ((0, "xq0.0"), (1, "x1.0"), (2, "x1.1"), (5, "wx.1"), (5, "wx.0"), (6, "xq0.1"), (6, "xq1.1"), (6, "xq1.0")),
+    6: ((1, "out1.0"), (8, "wx.3")),
+    7: ((0, "dz2.0"), (0, "dz2q.0"), (4, "out1.1"), (4, "wx.2"), (5, "out0.1"), (8, "out0.0")),
+}
+ENG = {"x": "v", "wx": "s", "out1.0": "sv", "out1.1": "sv", "out1.2": "ss", "out1.3": "ss", "dz2.0": "vv", "dz2.1": "sv", "out0.0": "svsv", "out0.1": "svss"}
+WPOS = (0, 2, 2, 2, 2, 2, 3, 3, 3, 3, 4, 5, 5, 6, 7, 7, 7, 8)
+PROLOGUE = ("hx0", "f1", "f2", "g0", "f0", "w0.0", "gv0.1", "gv0.0", "f8", "gv0.4", "gv0.2", "w0.1", "gv0.3", "w0.3", "f6", "gv0.6", "base0", "f4", "f7", "gv0.5", "f3", "f5", "w0.2", "f12", "w0.4", "gv0.7", "f10", "f14", "w0.5", "f9", "hx1", "f11", "f13", "f15", "f16", "f17", "g1")
+TAIL = ("sum", "fin", "dz2.1", "out1.2", "dz2q.1", "o0mm", "dzq", "o0tr", "out1.3")
 
 
 def tile_refiner_pa_v_kernel(tc, X, Y, Wx, bx, Wy, by, base_w, spline_w, spline_scaler, Hx, grad_out, out_0, out_1):
     nc = tc.nc
-    V, S, G, T = nc.vector, nc.scalar, nc.gpsimd, nc.tensor
+    V, S, T = nc.vector, nc.scalar, nc.tensor
     with ExitStack() as ctx:
         keep = ctx.enter_context(tc.tile_pool(name="keep", bufs=1))
         work = ctx.enter_context(tc.tile_pool(name="work", bufs=1))
@@ -61,8 +77,8 @@ def tile_refiner_pa_v_kernel(tc, X, Y, Wx, bx, Wy, by, base_w, spline_w, spline_
         def wt(shape, dt, tag, bufs):
             return work.tile(shape, dt, name=tag, tag=tag, bufs=bufs, align_bytes=64)
 
-        def bank(tag, bufs):
-            return psum.tile([P, 512], F32, name=tag, tag=tag, bufs=bufs)
+        def bank(tag):
+            return psum.tile([P, 512], F32, name=tag, tag=tag, bufs={"da": 4, "sum": 2, "misc": 2}[tag])
 
         def stage():
             return wt([P, 4096], BF16, "stage", 4)
@@ -70,46 +86,68 @@ def tile_refiner_pa_v_kernel(tc, X, Y, Wx, bx, Wy, by, base_w, spline_w, spline_
         def grp():
             return wt([P, 2048], BF16, "grp", 4)
 
+        def copy(engine, out, in_):
+            if engine == "v":
+                V.tensor_copy(out=out, in_=in_)
+            else:
+                S.copy(out=out, in_=in_)
+
         ident = kt([P, P], F32, "ident")
         warm = kt([P, 1], F32, "warm")
         V.memset(warm[:], 0.0)
-        S.activation(warm[:], warm[:], ACT.Sigmoid)
+        S.activation(warm[:], warm[:], ACT.Silu)
         make_identity(nc, ident[:])
 
         g_raw = stage()
+        hx = [kt([P, 4, 512], F32, "hx%d" % b) for b in range(2)]
+        sc = kt([P, 4, 512], BF16, "sc")
+        base = kt([P, 4, 512], BF16, "base")
+        sp = {}
 
         def load_g(b):
             nc.sync.dma_start(out=g_raw[:, b * 2048:(b + 1) * 2048].rearrange("p (j o) -> p j o", j=4),
                               in_=grad_out[b].rearrange("(p j) o -> p j o", j=4))
 
-        hx = [kt([P, 4, 512], F32, "hx%d" % b) for b in range(2)]
-        sc = kt([P, 4, 512], BF16, "sc")
-        base = kt([P, 4, 512], BF16, "base")
+        def load_hx(b, c0, c1):
+            nc.sync.dma_start(out=hx[b][:, :, c0:c1], in_=Hx[b * 512:(b + 1) * 512, c0:c1].rearrange("(p j) i -> p j i", j=4))
 
-        def load_hx(b):
-            nc.sync.dma_start(out=hx[b][:], in_=Hx[b * 512:(b + 1) * 512, :].rearrange("(p j) i -> p j i", j=4))
+        def load_sc(c0, c1):
+            nc.sync.dma_start(out=sc[:, :, c0:c1], in_=spline_scaler[:, c0:c1].rearrange("(p j) i -> p j i", j=4))
 
-        def load_sp(it):
-            t = stage()
-            nc.sync.dma_start(out=t[:].rearrange("p (j w) -> p j w", j=4),
-                              in_=spline_w[:, it * P:(it + 1) * P, :].rearrange("(p j) i k -> p j (i k)", j=4))
-            return t
+        def load_base(c0, c1):
+            nc.sync.dma_start(out=base[:, :, c0:c1], in_=base_w[:, c0:c1].rearrange("(p j) i -> p j i", j=4))
+
+        def load_sp(it, pieces):
+            if it not in sp:
+                sp[it] = stage()
+            for c0, c1 in pieces:
+                nc.sync.dma_start(out=sp[it][:].rearrange("p (j w) -> p j w", j=4)[:, :, 8 * c0:8 * c1],
+                                  in_=spline_w[:, it * P + c0:it * P + c1, :].rearrange("(p j) i k -> p j (i k)", j=4))
 
         def load_x(b):
             t = stage()
-            nc.sync.dma_start(out=t[:], in_=X[b].rearrange("t n f -> t (n f)"))
+            nc.sync.dma_start(out=t[:].rearrange("p (t r) -> p t r", r=32), in_=X[b].rearrange("t (p j) f -> p t (j f)", j=4))
             return t
 
-        sp = {}
+        def load_wx():
+            t = stage()
+            nc.sync.dma_start(out=t[:].rearrange("p (j w) -> p j w", j=4), in_=Wx.rearrange("(p j) w -> p j w", j=4))
+            return t
+
+        load_sc(0, 128)
+        load_hx(0, 0, 128)
+        load_sp(0, ((0, 64),))
         load_g(0)
-        load_hx(0)
-        nc.sync.dma_start(out=sc[:], in_=spline_scaler[:, 0:512].rearrange("(p j) i -> p j i", j=4))
-        sp[0] = load_sp(0)
-        nc.sync.dma_start(out=base[:], in_=base_w[:, 0:512].rearrange("(p j) i -> p j i", j=4))
+        load_sp(0, ((64, 128),))
+        load_base(0, 128)
         load_g(1)
-        load_hx(1)
-        sp[1] = load_sp(1)
-        sp[2] = load_sp(2)
+        load_hx(1, 0, 128)
+        load_sc(128, 512)
+        load_sp(1, ((0, 128),))
+        load_hx(0, 128, 512)
+        load_base(128, 512)
+        load_sp(2, ((0, 128),))
+        load_hx(1, 128, 512)
 
         gq = [kt([P, 1024], U32, "gq%d" % v) for v in range(4)]
         gs = [kt([P, 1024], U8, "gs%d" % v) for v in range(4)]
@@ -126,22 +164,20 @@ def tile_refiner_pa_v_kernel(tc, X, Y, Wx, bx, Wy, by, base_w, spline_w, spline_
         vq = kt([P, 1024], U32, "vq")
         vs = kt([P, 1024], U8, "vs")
         dz = [kt([P, 512, 4], BF16, "dz%d" % b) for b in range(2)]
+        task = {}
 
         def g_transposes(b):
             words = g_raw[:].bitcast(F32)
             gg = wt([P, 2048], BF16, "gg", 1)
             ggw = gg[:].bitcast(F32)
             for h in range(2):
-                pt = bank("misc", 2)
+                pt = bank("misc")
                 for jj in range(2):
                     for u in range(2):
                         w0 = (b * 4 + 2 * h + jj) * 256
                         T.transpose(pt[:, (2 * jj + u) * P:(2 * jj + u + 1) * P], words[:, w0 + u:w0 + 256:2], ident[:])
                 S.copy(out=ggw[:, h * 512:(h + 1) * 512].rearrange("c (j p u) -> c j p u", j=2, u=2),
                        in_=pt[:].rearrange("c (j u p) -> c j p u", j=2, u=2))
-            return gg
-
-        def g_variants_steps(b, gg):
             cols = slice(b * 512, (b + 1) * 512)
             tiles = {}
 
@@ -155,29 +191,29 @@ def tile_refiner_pa_v_kernel(tc, X, Y, Wx, bx, Wy, by, base_w, spline_w, spline_
                 def run():
                     V.quantize_mx(out=gq[v][:, cols].bitcast(E5), scales=gs[v][:, cols], in_=tiles[v][:])
                 return run
-            return [scaled(0), scaled(1), quant(0), scaled(2), quant(1), scaled(3), quant(2), quant(3)]
+            for k, step in enumerate((scaled(0), scaled(1), quant(0), scaled(2), quant(1), scaled(3), quant(2), quant(3))):
+                task["gv%d.%d" % (b, k)] = step
 
-        def g_variants(b, gg):
-            for step in g_variants_steps(b, gg):
-                step()
+        def base_task(it):
+            def run():
+                isl = slice(it * P, (it + 1) * P)
+                t = wt([P, P, 4], BF16, "bg", 1)
+                S.copy(out=t[:], in_=base[:, :, isl].rearrange("p j w -> p w j"))
+                V.quantize_mx(out=bq[:, isl].bitcast(E4), scales=bs[:, isl], in_=t[:].rearrange("p w j -> p (w j)"))
+            return run
 
-        def w2_base():
-            t = grp()
-            S.copy(out=t[:].rearrange("p (w j) -> p w j", j=4), in_=base[:].rearrange("p j w -> p w j"))
-            V.quantize_mx(out=bq[:].bitcast(E4), scales=bs[:], in_=t[:])
-
-        def w2_pieces(it):
-            raw = sp[it][:].rearrange("p (j q k) -> p k q j", j=4, k=8)
-            fac = sc[:, :, it * P:(it + 1) * P].rearrange("p j q -> p q j")
+        def w2_tasks(it):
             tiles = {}
 
             def product(h, half):
                 def run():
+                    raw = sp[it][:].rearrange("p (j q k) -> p q k j", j=4, k=8)
+                    fac = sc[:, :, it * P:(it + 1) * P].rearrange("p j q -> p q j")
                     if half == 0:
                         tiles[h] = grp()
-                    k0 = 4 * h + 2 * half
-                    V.tensor_tensor(out=tiles[h][:, half * 1024:(half + 1) * 1024].rearrange("p (k q j) -> p k q j", k=2, j=4),
-                                    in0=raw[:, k0:k0 + 2], in1=fac.unsqueeze(1).to_broadcast([P, 2, P, 4]), op=ALU.mult)
+                    qs = slice(64 * half, 64 * half + 64)
+                    V.tensor_tensor(out=tiles[h][:].rearrange("p (k q j) -> p q k j", k=4, j=4)[:, qs],
+                                    in0=raw[:, qs, 4 * h:4 * h + 4], in1=fac[:, qs].unsqueeze(2).to_broadcast([P, 64, 4, 4]), op=ALU.mult)
                 return run
 
             def quant(h):
@@ -185,79 +221,68 @@ def tile_refiner_pa_v_kernel(tc, X, Y, Wx, bx, Wy, by, base_w, spline_w, spline_
                     cols = slice(h * 512, (h + 1) * 512)
                     V.quantize_mx(out=wq[it][:, cols].bitcast(E4), scales=ws[it][:, cols], in_=tiles[h][:])
                 return run
-            return [product(0, 0), product(0, 1), product(1, 0), quant(0), product(1, 1), quant(1)]
+            for k, step in enumerate((product(0, 0), product(0, 1), product(1, 0), quant(0), product(1, 1), quant(1))):
+                task["w%d.%d" % (it, k)] = step
+
+        for it in range(4):
+            task["base%d" % it] = base_task(it)
+            w2_tasks(it)
 
         ht = {}
 
         def hx_transposes(n):
             it, b = ORDER[n]
-            pt = bank("misc", 2)
+            pt = bank("misc")
             for j in range(4):
                 T.transpose(pt[:, j * P:(j + 1) * P], hx[b][:, j, it * P:(it + 1) * P], ident[:])
             ht[n] = wt([P, 512], F32, "ht", 2)
             S.copy(out=ht[n][:], in_=pt[:])
 
         wgt = {}
-        tmp = {}
 
         def weights(n):
             h = ht[n]
             w = {}
-            steps = {}
-
-            def sigmoid():
-                tmp[n] = wt([P, 512], F32, "sg", 1)
-                S.activation(tmp[n][:], h[:], ACT.Sigmoid)
-
-            def silu_a():
-                w["S"] = wt([P, 512], F32, "wS", 2)
-                V.scalar_tensor_tensor(out=w["S"][:], in0=tmp[n][:], scalar=1.0, in1=h[:], op0=ALU.subtract, op1=ALU.mult)
-
-            def silu_b():
-                V.scalar_tensor_tensor(out=w["S"][:], in0=w["S"][:], scalar=1.0, in1=tmp[n][:], op0=ALU.subtract, op1=ALU.mult)
-
-            def dist(j):
-                def run():
-                    w["s%d" % j] = wt([P, 512], F32, "ws%d" % j, 2)
-                    S.activation(w["s%d" % j][:], h[:], ACT.Abs, bias=6.25 - 2.5 * j, scale=6.25)
-                return run
-
-            def signed(j):
-                def run():
-                    t = w["s%d" % j]
-                    V.scalar_tensor_tensor(out=t[:], in0=h[:], scalar=0.4 * j - 1.0, in1=t[:], op0=ALU.subtract, op1=ALU.mult)
-                return run
-
-            def relu(side, j):
-                def run():
-                    t = wt([P, 512], F32, "w%s%d" % (side, j), 2)
-                    w["%s%d" % (side, j)] = t
-                    sign = 1.0 if side == "R" else -1.0
-                    S.activation(t[:], h[:], ACT.Relu, bias=sign * (2.5 - j), scale=sign * 2.5)
-                return run
-
-            def square_(side, j):
-                def run():
-                    t = w["%s%d" % (side, j)]
-                    S.activation(t[:], t[:], ACT.Square)
-                return run
             wgt[n] = w
-            return {0: [sigmoid, relu("L", 2)], 1: [dist(3), square_("L", 2), relu("R", 2)], 2: [silu_a, square_("R", 2), relu("L", 1)], 3: [signed(3), square_("L", 1), relu("R", 1)],
-                    4: [silu_b, square_("R", 1), relu("L", 4)], 5: [square_("L", 4)], 6: [relu("R", 4)], 7: [square_("R", 4)]}
+
+            def act(name, func, scale, bias=0.0):
+                def run():
+                    w[name] = wt([P, 512], F32, "w" + name, 2)
+                    S.activation(w[name][:], h[:], func, bias=bias, scale=scale)
+                return run
+
+            def relu(name):
+                sign = 1.0 if name[0] == "R" else -1.0
+                return act(name, ACT.Relu, sign * 2.5, sign * (2.5 - int(name[1])))
+
+            def square(name):
+                def run():
+                    S.activation(w[name][:], w[name][:], ACT.Square, scale=math.sqrt(2.5))
+                return run
+
+            steps = [act("T", ACT.Tanh, -0.5), act("U", ACT.Silu, -1.0)]
+            for name in ("L2", "R2", "L3", "R3", "L1", "R1", "L4", "R4"):
+                steps += [relu(name), square(name)]
+            for k, s in enumerate(steps):
+                task["f%d" % k] = s
+            d = {}
+            for k, s in zip(WPOS, steps):
+                d.setdefault(k, []).append(s)
+            return d
 
         sqs = {}
 
-        def square(n):
+        def hx_square(n):
             it, b = ORDER[n]
             sqs[n] = wt([P, 4, P], F32, "sq", 2)
-            S.activation(sqs[n][:], hx[b][:, :, it * P:(it + 1) * P], ACT.Square, scale=math.sqrt(1.25))
+            S.activation(sqs[n][:], hx[b][:, :, it * P:(it + 1) * P], ACT.Square, scale=math.sqrt(0.5))
 
         prod = {}
 
-        def term_passes(n, r):
+        def term(n, r):
             it, b = ORDER[n]
             name, op, const, passes = TERMS[r]
-            da = bank("da", 4)
+            da = bank("da")
             cols = slice(b * 512, (b + 1) * 512)
             for s, (c, v) in enumerate(passes):
                 if c == 0:
@@ -266,24 +291,27 @@ def tile_refiner_pa_v_kernel(tc, X, Y, Wx, bx, Wy, by, base_w, spline_w, spline_
                     lq, ls = wq[it][:, (c - 1) * P:c * P], ws[it][:, (c - 1) * P:c * P]
                 T.matmul_mx(out=da[:], lhsT=lq.bitcast(E4), lhsT_scale=ls, rhs=gq[v][:, cols].bitcast(E5), rhs_scale=gs[v][:, cols],
                             start=(s == 0), stop=(s == len(passes) - 1))
-            pr = wt([P, 512], F32, "prod", 14)
+            pr = wt([P, 512], F32, "prod", PRODS)
             V.scalar_tensor_tensor(out=pr[:], in0=wgt[n][name][:], scalar=const, in1=da[:], op0=OPS[op], op1=ALU.mult)
             prod[n, r] = pr
+
+        def silu_second(n):
+            pr = prod[n, 0]
+            V.scalar_tensor_tensor(out=pr[:], in0=wgt[n]["U"][:], scalar=1.0, in1=pr[:], op0=ALU.subtract, op1=ALU.mult)
 
         sums = {}
 
         def sum_transposes(n):
-            sm = bank("sum", 2)
+            sm = bank("sum")
             for j in range(4):
                 js = slice(j * P, (j + 1) * P)
-                for r in range(len(TERMS)):
-                    T.matmul(sm[:, js], lhsT=prod[n, r][:, js], rhs=ident[:], is_transpose=True, start=(r == 0), stop=(r == len(TERMS) - 1))
+                for r in range(NT):
+                    T.matmul(sm[:, js], lhsT=prod[n, r][:, js], rhs=ident[:], is_transpose=True, start=(r == 0), stop=(r == NT - 1))
             sums[n] = sm
 
         def dz_final(n):
             it, b = ORDER[n]
-            sq = sqs[n]
-            V.scalar_tensor_tensor(out=dz[b][:, it * P:(it + 1) * P, :], in0=sq[:].rearrange("p j q -> p q j"), scalar=1.25,
+            V.scalar_tensor_tensor(out=dz[b][:, it * P:(it + 1) * P, :], in0=sqs[n][:].rearrange("p j q -> p q j"), scalar=0.5,
                                    in1=sums[n][:].rearrange("p (j q) -> p q j", j=4), op0=ALU.subtract, op1=ALU.mult)
 
         def dz_quant(n):
@@ -291,178 +319,164 @@ def tile_refiner_pa_v_kernel(tc, X, Y, Wx, bx, Wy, by, base_w, spline_w, spline_
             isl = slice(it * P, (it + 1) * P)
             V.quantize_mx(out=dq[b][:, isl].bitcast(E5), scales=ds[b][:, isl], in_=dz[b][:, isl, :].rearrange("p q j -> p (q j)"))
 
-        def dz2(b, copies):
-            words = dz[b][:].rearrange("p i j -> p (i j)").bitcast(F32)
-            t2 = grp()
-            for v in range(2):
-                pt = bank("misc", 2)
-                for t in range(4):
-                    T.transpose(pt[:, t * P:(t + 1) * P], words[:, 2 * t + v::8], ident[:])
-                dst = t2[:, v * 1024:(v + 1) * 1024].rearrange("c (e p t) -> c e p t", e=2, t=4)
-                src = pt[:].bitcast(BF16).rearrange("c (t p e) -> c e p t", t=4, e=2)
-                if copies[v] == "v":
-                    V.tensor_copy(out=dst, in_=src)
-                else:
-                    S.copy(out=dst, in_=src)
-            return t2
+        dzt = {}
 
-        def dz2_quant(b, t2):
-            V.quantize_mx(out=eq[b][:].bitcast(E5), scales=es[b][:], in_=t2[:])
+        def dz2(b):
+            def run():
+                words = dz[b][:].rearrange("p i j -> p (i j)").bitcast(F32)
+                dzt[b] = grp()
+                for v in range(2):
+                    pt = bank("misc")
+                    for t in range(4):
+                        T.transpose(pt[:, t * P:(t + 1) * P], words[:, 2 * t + v::8], ident[:])
+                    copy(ENG["dz2.%d" % b][v], dzt[b][:, v * 1024:(v + 1) * 1024].rearrange("c (e p t) -> c e p t", e=2, t=4),
+                         pt[:].bitcast(BF16).rearrange("c (t p e) -> c e p t", t=4, e=2))
+            return run
 
-        def wx_prep():
-            raw = stage()
-            nc.sync.dma_start(out=raw[:].rearrange("p (j w) -> p j w", j=4), in_=Wx.rearrange("(p j) w -> p j w", j=4))
-            rv = raw[:].rearrange("p (j w) -> p w j", j=4)
-            tiles = [grp(), grp()]
+        def dz2_quant(b):
+            def run():
+                V.quantize_mx(out=eq[b][:].bitcast(E5), scales=es[b][:], in_=dzt[b][:])
+            return run
 
-            def cp(h):
-                def run():
-                    S.copy(out=tiles[h][:].rearrange("p (w j) -> p w j", j=4), in_=rv[:, h * 512:(h + 1) * 512, :])
-                return run
+        raws = {}
+        wxt = {}
 
-            def qn(h):
-                def run():
-                    V.quantize_mx(out=vq[:, h * 512:(h + 1) * 512].bitcast(E4), scales=vs[:, h * 512:(h + 1) * 512], in_=tiles[h][:])
-                return run
-            return [cp(0), cp(1), qn(0), qn(1)]
+        def wx_copy(h):
+            def run():
+                wxt[h] = grp()
+                copy(ENG["wx"], wxt[h][:].rearrange("p (w j) -> p w j", j=4), raws["wx"][:].rearrange("p (j w) -> p w j", j=4)[:, h * 512:(h + 1) * 512, :])
+            return run
+
+        def wx_quant(h):
+            def run():
+                V.quantize_mx(out=vq[:, h * 512:(h + 1) * 512].bitcast(E4), scales=vs[:, h * 512:(h + 1) * 512], in_=wxt[h][:])
+            return run
 
         xg = {}
 
-        def x_bank(b, xt, w):
-            if w == 0:
-                xg[b] = wt([P, 4096], BF16, "ot", 2)
-            words = xt[:].bitcast(F32)
-            pt = bank("misc", 2)
+        def x_copy(b, h):
+            def run():
+                xg[b, h] = grp()
+                copy(ENG["x"], xg[b, h][:].rearrange("p (t f j) -> p t f j", f=8, j=4),
+                     raws["x%d" % b][:].rearrange("p (t j f) -> p t f j", j=4, f=8)[:, h * 64:(h + 1) * 64])
+            return run
+
+        def x_quant(b, h):
+            def run():
+                cols = slice(h * 512, (h + 1) * 512)
+                V.quantize_mx(out=xq[b][:, cols].bitcast(E4), scales=xs[b][:, cols], in_=xg[b, h][:])
+            return run
+
+        def out1(it):
+            def run():
+                o = wt([P, 2048], F32, "ot", 2)
+                for h in range(2):
+                    pt = bank("misc")
+                    for b in range(2):
+                        T.matmul_mx(out=pt[:], lhsT=dq[b][:, it * P:(it + 1) * P].bitcast(E5), lhsT_scale=ds[b][:, it * P:(it + 1) * P],
+                                    rhs=xq[b][:, h * 512:(h + 1) * 512].bitcast(E4), rhs_scale=xs[b][:, h * 512:(h + 1) * 512],
+                                    start=(b == 0), stop=(b == 1))
+                    copy(ENG["out1.%d" % it][h], o[:, h * 512:(h + 1) * 512], pt[:])
+                nc.sync.dma_start(out=out_1[it * P:(it + 1) * P, :], in_=o[:, 0:1024])
+            return run
+
+        def out0_matmul(b, j, h, tag):
+            pt = bank(tag)
+            T.matmul_mx(out=pt[:], lhsT=eq[b][:, j * P:(j + 1) * P].bitcast(E5), lhsT_scale=es[b][:, j * P:(j + 1) * P],
+                        rhs=vq[:, h * 512:(h + 1) * 512].bitcast(E4), rhs_scale=vs[:, h * 512:(h + 1) * 512], start=True, stop=True)
+            return pt
+
+        def out0(b, h):
+            def run():
+                o = wt([P, 2048], F32, "ot", 2)
+                ov = o[:].rearrange("p (t j f) -> p t j f", j=4, f=8)
+                for j in range(4):
+                    pt = out0_matmul(b, j, h, "misc")
+                    copy(ENG["out0.%d" % h][j], ov[:, :, j, :], pt[:].rearrange("p (t f) -> p t f", f=8))
+                nc.sync.dma_start(out=out_0[b, h * 64:(h + 1) * 64].rearrange("t (p j) f -> p t (j f)", j=4), in_=o[:].rearrange("p (t r) -> p t r", r=32))
+            return run
+
+        def out0_flat(b):
+            flat = []
             for j in range(4):
-                T.transpose(pt[:, j * P:(j + 1) * P], words[:, 4 * j + w::16], ident[:])
-            S.copy(out=xg[b][:].rearrange("p (t f j) -> p t f j", f=8, j=4)[:, :, 2 * w:2 * w + 2, :],
-                   in_=pt[:].bitcast(BF16).rearrange("p (j t e) -> p t e j", j=4, e=2))
+                if j % 2 == 0:
+                    o = stage()[:].bitcast(F32)
+                oj = o[:, (j % 2) * 1024:(j % 2 + 1) * 1024].rearrange("p (f t) -> p f t", f=8)
+                for h in range(2):
+                    pt = out0_matmul(b, j, h, "misc" if h else "da")
+                    copy("v" if h else "s", oj[:, :, h * 64:(h + 1) * 64], pt[:].rearrange("p (t f) -> p f t", f=8))
+                flat.append(oj)
+            return flat
 
-        def x_quant(b):
-            V.quantize_mx(out=xq[b][:].bitcast(E4), scales=xs[b][:], in_=xg[b][:])
+        def out0_by_t(b, flat):
+            halves = [stage()[:].bitcast(F32).rearrange("t (p j f) -> t p j f", j=4, f=8) for half in range(2)]
+            for j in range(4):
+                for g in range(2):
+                    pt = bank("misc" if g else "da")
+                    for f in range(4):
+                        T.transpose(pt[:, f * P:(f + 1) * P], flat[j][:, 4 * g + f, :], ident[:])
+                    src = pt[:].rearrange("t (f p) -> t p f", f=4)
+                    for half in range(2):
+                        copy("v" if g else "s", halves[half][:, :, j, 4 * g:4 * g + 4], src[:, half * 64:(half + 1) * 64])
+            for half in range(2):
+                nc.sync.dma_start(out=out_0[b, :, half * 256:(half + 1) * 256, :].rearrange("t (p j) f -> t p j f", j=4), in_=halves[half])
 
-        def out_tile(tail):
-            return stage()[:].bitcast(F32) if tail else wt([P, 2048], F32, "ot", 2)[:]
-
-        def out1(it, engines, tail=False):
-            o = out_tile(tail)
+        for h in range(2):
+            task["wx.%d" % h] = wx_copy(h)
+            task["wx.%d" % (2 + h)] = wx_quant(h)
+            task["out0.%d" % h] = out0(0, h)
+        for b in range(2):
             for h in range(2):
-                pt = bank("misc", 2)
-                for b in range(2):
-                    T.matmul_mx(out=pt[:], lhsT=dq[b][:, it * P:(it + 1) * P].bitcast(E5), lhsT_scale=ds[b][:, it * P:(it + 1) * P],
-                                rhs=xq[b][:, h * 512:(h + 1) * 512].bitcast(E4), rhs_scale=xs[b][:, h * 512:(h + 1) * 512],
-                                start=(b == 0), stop=(b == 1))
-                if engines[h] == "v":
-                    V.tensor_copy(out=o[:, h * 512:(h + 1) * 512], in_=pt[:])
-                else:
-                    S.copy(out=o[:, h * 512:(h + 1) * 512], in_=pt[:])
-            nc.sync.dma_start(out=out_1[it * P:(it + 1) * P, :], in_=o[:, 0:1024])
+                task["x%d.%d" % (b, h)] = x_copy(b, h)
+                task["xq%d.%d" % (b, h)] = x_quant(b, h)
+            task["dz2.%d" % b] = dz2(b)
+            task["dz2q.%d" % b] = dz2_quant(b)
+        for it in range(4):
+            task["out1.%d" % it] = out1(it)
 
-        def out0(b, h, engines, tail=False):
-            o = out_tile(tail)
-            ov = o.rearrange("p (t j f) -> p t j f", j=4, f=8)
-            for j in range(4):
-                pt = bank("misc", 2)
-                T.matmul_mx(out=pt[:], lhsT=eq[b][:, j * P:(j + 1) * P].bitcast(E5), lhsT_scale=es[b][:, j * P:(j + 1) * P],
-                            rhs=vq[:, h * 512:(h + 1) * 512].bitcast(E4), rhs_scale=vs[:, h * 512:(h + 1) * 512], start=True, stop=True)
-                src = pt[:].rearrange("p (t f) -> p t f", f=8)
-                if engines[j] == "v":
-                    V.tensor_copy(out=ov[:, :, j, :], in_=src)
-                else:
-                    S.copy(out=ov[:, :, j, :], in_=src)
-            nc.sync.dma_start(out=out_0[b, h * 64:(h + 1) * 64].rearrange("t (p j) f -> p t (j f)", j=4),
-                              in_=o.rearrange("p (t r) -> p t r", r=32))
+        task["hx0"] = lambda: (hx_transposes(0), weights(0))
+        task["hx1"] = lambda: hx_transposes(1)
+        task["g0"] = lambda: g_transposes(0)
+        task["g1"] = lambda: g_transposes(1)
+        for name in PROLOGUE:
+            task[name]()
 
-        gg0 = g_transposes(0)
-        hx_transposes(0)
-        first = weights(0)
-        for k in (0, 1):
-            for step in first[k]:
-                step()
-        g_variants(0, gg0)
-        pieces = w2_pieces(0)
-        w2_base()
-        pieces[0]()
-        for k in (2, 3):
-            for step in first[k]:
-                step()
-        pieces[1]()
-        pieces[2]()
-        for k in (4, 5, 6, 7):
-            for step in first[k]:
-                step()
-        for step in pieces[3:]:
-            step()
-        gg1 = g_transposes(1)
-        hx_transposes(1)
-
-        xt = {}
-        t2 = {}
-
-        def slot(n, tasks):
-            for r in range(len(TERMS)):
-                term_passes(n, r)
-                for task in tasks.get(r, ()):
-                    task()
+        for n in range(len(ORDER)):
+            d = weights(n + 1) if n + 1 < len(ORDER) else {}
+            if n == 1:
+                load_sp(3, ((0, 128),))
+            elif n == 2:
+                raws["x0"] = load_x(0)
+            elif n == 3:
+                raws["x1"] = load_x(1)
+            elif n == 5:
+                raws["wx"] = load_wx()
+            for r in range(NT):
+                term(n, r)
+                for k, name in PLAN[n]:
+                    if k == r:
+                        task[name]()
+                for step in d.get(r, ()):
+                    step()
+                if r == 1:
+                    silu_second(n)
                 if r == SUM_AT:
                     if n > 0:
                         sum_transposes(n - 1)
                     if n + 2 < len(ORDER):
                         hx_transposes(n + 2)
-                if n > 0 and r == SUM_AT + 1:
-                    dz_final(n - 1)
                 if r == SUM_AT + 1:
-                    square(n)
+                    if n > 0:
+                        dz_final(n - 1)
+                    hx_square(n)
                 if n > 0 and r == SUM_AT + 2:
                     dz_quant(n - 1)
 
-        def merge(*maps):
-            d = {}
-            for m in maps:
-                for k, v in m.items():
-                    d.setdefault(k, []).extend(v)
-            return d
-
-        def spread(steps, where):
-            d = {}
-            for k, s in zip(where, steps):
-                d.setdefault(k, []).append(s)
-            return d
-
-        def xb(b, w):
-            return lambda: x_bank(b, xt[b], w)
-
-        for n in range(len(ORDER)):
-            nxt = weights(n + 1) if n + 1 < len(ORDER) else {}
-            extra = {}
-            if n == 0:
-                extra = spread(g_variants_steps(1, gg1), (0, 1, 2, 3, 4, 5, 6, 7))
-            elif n == 1:
-                extra = spread(w2_pieces(1), (0, 1, 3, 5, 6, 7))
-                steps = wx_prep()
-                xt[0] = load_x(0)
-            elif n == 2:
-                extra = merge(spread(w2_pieces(2), (0, 1, 3, 5, 6, 7)), spread([xb(0, 0), xb(0, 1)], (2, 7)))
-                sp[3] = load_sp(3)
-            elif n == 3:
-                extra = merge(spread(steps, (0, 2, 4, 6)), spread([xb(0, 2), xb(0, 3)], (1, 7)))
-                xt[1] = load_x(1)
-            elif n == 4:
-                extra = merge(spread(w2_pieces(3), (0, 1, 3, 5, 6, 7)), spread([xb(1, 0), xb(1, 1)], (2, 7)), {8: [lambda: x_quant(0)]})
-            elif n == 5:
-                extra = merge(spread([xb(1, 2), xb(1, 3)], (1, 3)), {5: [lambda: x_quant(1)], 6: [lambda: out1(0, "ss")]})
-            elif n == 6:
-                extra = {6: [lambda: t2.setdefault(0, dz2(0, "ss"))], 7: [lambda: dz2_quant(0, t2[0])], 8: [lambda: out0(0, 0, "ssss")]}
-            elif n == 7:
-                extra = {2: [lambda: out0(0, 1, "ssss")], 7: [lambda: out1(1, "ss")]}
-            slot(n, merge(extra, nxt))
-
-        sum_transposes(7)
-        out1(2, "vs", True)
-        dz_final(7)
-        t2[1] = dz2(1, "vs")
-        dz2_quant(1, t2[1])
-        dz_quant(7)
-        out0(1, 0, "vsvs", True)
-        out0(1, 1, "vsvs", True)
-        out1(3, "vs", True)
+        task["sum"] = lambda: sum_transposes(7)
+        task["fin"] = lambda: dz_final(7)
+        task["dzq"] = lambda: dz_quant(7)
+        flat = []
+        task["o0mm"] = lambda: flat.extend(out0_flat(1))
+        task["o0tr"] = lambda: out0_by_t(1, flat)
+        for name in TAIL:
+            task[name]()

@@ -12,16 +12,16 @@ E4 = mybir.dt.float8_e4m3fn_x4
 E5 = mybir.dt.float8_e5m2_x4
 ALU = mybir.AluOpType
 ACT = mybir.ActivationFunctionType
-OPS = {"sub": ALU.subtract, "mult": ALU.mult, "min": ALU.min, "max": ALU.max}
+OPS = {"add": ALU.add, "mult": ALU.mult}
 
 FLOPS = 2 * 1024 * 512 * 4608 + 2 * 2 * 1024 * 512 * 1024
 BYTES = 2 * (1048576 + 524288 + 262144 + 2097152 + 262144 + 524288) + 4 * (524288 + 1048576 + 524288)
 
 P = 128
 SUM_AT = 4
-NEG, POS4, NEG4, NEG2 = 0, 1, 2, 3
-VARIANT = (-1.0, 4.0, -4.0, -2.0)
-CHAIN = ((NEG,), (POS4,), (NEG4, NEG2), (POS4,))
+POS, NEG4, POS4, POS2 = 0, 1, 2, 3
+VARIANT = (1.0, -4.0, 4.0, 2.0)
+CHAIN = ((POS,), (NEG4,), (POS4, POS2), (NEG4,))
 
 
 def left(j):
@@ -33,33 +33,35 @@ def right(j):
 
 
 TERMS = (
-    ("T", "sub", 1.0, ((0, NEG),)),
-    ("L2", "mult", -1.0, left(2)),
-    ("R2", "mult", 1.0, right(2)),
-    ("L3", "mult", -1.0, left(3)),
-    ("R3", "mult", 1.0, right(3)),
-    ("L1", "mult", -1.0, left(1)),
-    ("R1", "mult", 1.0, right(1)),
-    ("L4", "mult", -1.0, left(4)),
-    ("R4", "mult", 1.0, right(4)),
+    ("T", "add", 1.0, ((0, POS),)),
+    ("L2", "mult", 1.0, left(2)),
+    ("R2", "mult", -1.0, right(2)),
+    ("L3", "mult", 1.0, left(3)),
+    ("R3", "mult", -1.0, right(3)),
+    ("L1", "mult", 1.0, left(1)),
+    ("R1", "mult", -1.0, right(1)),
+    ("L4", "mult", 1.0, left(4)),
+    ("R4", "mult", -1.0, right(4)),
 )
 NT = len(TERMS)
-PRODS = 10
+PRODS = 16
+WGTS = 14
+KNOTS = ("L2", "R2", "L3", "R3", "L1", "R1", "L4", "R4")
 ORDER = ((0, 0), (0, 1), (1, 0), (2, 0), (1, 1), (3, 0), (2, 1), (3, 1))
 PLAN = {
-    0: ((0, "gv1.0"), (0, "gv1.3"), (0, "gv1.2"), (1, "gv1.5"), (3, "gv1.1"), (3, "w1.0"), (4, "gv1.4"), (6, "w1.2"), (6, "gv1.7"), (6, "gv1.6"), (6, "base1")),
-    1: ((1, "w2.0"), (1, "w1.4"), (1, "w2.1"), (1, "w1.1"), (3, "base2"), (4, "w1.3"), (6, "base3"), (6, "w1.5"), (7, "w2.3")),
-    2: ((1, "w2.2"), (2, "w2.4"), (4, "w2.5"), (8, "w3.0")),
-    3: ((1, "x0.0"), (2, "w3.1"), (3, "w3.3")),
-    4: ((0, "w3.2"), (1, "w3.4"), (2, "x0.1"), (7, "w3.5")),
-    5: ((0, "xq0.0"), (1, "x1.0"), (2, "x1.1"), (5, "wx.1"), (5, "wx.0"), (6, "xq0.1"), (6, "xq1.1"), (6, "xq1.0")),
-    6: ((1, "out1.0"), (8, "wx.3")),
-    7: ((0, "dz2.0"), (0, "dz2q.0"), (4, "out1.1"), (4, "wx.2"), (5, "out0.1"), (8, "out0.0")),
+    0: ((0, "w1.0"), (0, "gv1.1"), (0, "gv1.0"), (1, "gv1.4"), (1, "base1"), (2, "gv1.6"), (2, "gv1.2"), (3, "gv1.3"), (6, "w1.1"), (6, "w1.2"), (6, "base2"), (7, "gv1.5"), (8, "w1.3")),
+    1: ((2, "w1.4"), (3, "w2.0"), (4, "w1.5"), (4, "base3"), (7, "w2.1")),
+    2: ((0, "w2.2"), (1, "w2.4"), (1, "w3.0"), (3, "w2.5"), (4, "w2.3")),
+    3: ((1, "x0.0"), (1, "w3.1"), (3, "w3.2")),
+    4: ((0, "w3.4"), (3, "x0.1"), (3, "w3.5"), (4, "w3.3")),
+    5: ((0, "x1.0"), (0, "x1.1"), (3, "xq1.0"), (4, "xq0.0"), (6, "xq0.1"), (6, "xq1.1")),
+    6: ((1, "out1.0"), (7, "out1.1")),
+    7: ((1, "dz2.00"), (1, "dz2.01"), (1, "dz2q.01"), (1, "wx.1"), (2, "wx.0"), (4, "dz2q.00"), (4, "wx.3"), (4, "wx.2"), (5, "out0.1"), (8, "out0.0")),
 }
-ENG = {"x": "v", "wx": "s", "out1.0": "sv", "out1.1": "sv", "out1.2": "ss", "out1.3": "ss", "dz2.0": "vv", "dz2.1": "sv", "out0.0": "svsv", "out0.1": "svss"}
-WPOS = (0, 2, 2, 2, 2, 2, 3, 3, 3, 3, 4, 5, 5, 6, 7, 7, 7, 8)
-PROLOGUE = ("hx0", "f1", "f2", "g0", "f0", "w0.0", "gv0.1", "gv0.0", "f8", "gv0.4", "gv0.2", "w0.1", "gv0.3", "w0.3", "f6", "gv0.6", "base0", "f4", "f7", "gv0.5", "f3", "f5", "w0.2", "f12", "w0.4", "gv0.7", "f10", "f14", "w0.5", "f9", "hx1", "f11", "f13", "f15", "f16", "f17", "g1")
-TAIL = ("sum", "fin", "dz2.1", "out1.2", "dz2q.1", "o0mm", "dzq", "o0tr", "out1.3")
+ENG = {"x": "v", "wx": "s", "out1.0": "vs", "out1.1": "vs", "out1.2": "ss", "out1.3": "vs", "dz2.0": "vv", "dz2.1": "vs", "out0.0": "svvv", "out0.1": "vsss"}
+WPOS = (0, 0, 1, 1, 1, 2, 3, 3, 3, 3, 4, 4, 5, 6, 6, 8, 8, 8)
+PROLOGUE = ("w0.0", "hx0", "f0", "w0.1", "f1", "g0", "gv0.2", "f2", "gv0.1", "f3", "w0.2", "f4", "gv0.3", "f5", "w0.4", "w0.3", "f6", "gv0.0", "f7", "f8", "f9", "gv0.4", "f10", "gv0.5", "base0", "w0.5", "f11", "f12", "hx1", "f13", "gv0.6", "f14", "g1", "f15", "f16", "f17")
+TAIL = ("sum0", "fin0", "dz2.10", "sum2", "fin2", "dz2.11", "dz2q.10", "mm0", "dz2q.11", "mm1", "mm2", "mm3", "tr0", "tr1", "tr2", "tr3", "store", "dzq", "out1.3", "out1.2")
 
 
 def tile_refiner_pa_v_kernel(tc, X, Y, Wx, bx, Wy, by, base_w, spline_w, spline_scaler, Hx, grad_out, out_0, out_1):
@@ -81,7 +83,7 @@ def tile_refiner_pa_v_kernel(tc, X, Y, Wx, bx, Wy, by, base_w, spline_w, spline_
             return psum.tile([P, 512], F32, name=tag, tag=tag, bufs={"da": 4, "sum": 2, "misc": 2}[tag])
 
         def stage():
-            return wt([P, 4096], BF16, "stage", 4)
+            return wt([P, 4096], BF16, "stage", 3)
 
         def grp():
             return wt([P, 2048], BF16, "grp", 4)
@@ -100,8 +102,8 @@ def tile_refiner_pa_v_kernel(tc, X, Y, Wx, bx, Wy, by, base_w, spline_w, spline_
 
         g_raw = stage()
         hx = [kt([P, 4, 512], F32, "hx%d" % b) for b in range(2)]
-        sc = kt([P, 4, 512], BF16, "sc")
-        base = kt([P, 4, 512], BF16, "base")
+        sc = {}
+        base = {}
         sp = {}
 
         def load_g(b):
@@ -111,11 +113,15 @@ def tile_refiner_pa_v_kernel(tc, X, Y, Wx, bx, Wy, by, base_w, spline_w, spline_
         def load_hx(b, c0, c1):
             nc.sync.dma_start(out=hx[b][:, :, c0:c1], in_=Hx[b * 512:(b + 1) * 512, c0:c1].rearrange("(p j) i -> p j i", j=4))
 
-        def load_sc(c0, c1):
-            nc.sync.dma_start(out=sc[:, :, c0:c1], in_=spline_scaler[:, c0:c1].rearrange("(p j) i -> p j i", j=4))
+        def load_rows(name, store, it, src):
+            store[it] = wt([P, 4, P], BF16, name, 4 if name == "base" else 2)
+            nc.sync.dma_start(out=store[it][:], in_=src[:, it * P:(it + 1) * P].rearrange("(p j) i -> p j i", j=4))
 
-        def load_base(c0, c1):
-            nc.sync.dma_start(out=base[:, :, c0:c1], in_=base_w[:, c0:c1].rearrange("(p j) i -> p j i", j=4))
+        def load_sc(it):
+            load_rows("sc", sc, it, spline_scaler)
+
+        def load_base(it):
+            load_rows("base", base, it, base_w)
 
         def load_sp(it, pieces):
             if it not in sp:
@@ -134,20 +140,22 @@ def tile_refiner_pa_v_kernel(tc, X, Y, Wx, bx, Wy, by, base_w, spline_w, spline_
             nc.sync.dma_start(out=t[:].rearrange("p (j w) -> p j w", j=4), in_=Wx.rearrange("(p j) w -> p j w", j=4))
             return t
 
-        load_sc(0, 128)
+        load_sc(0)
         load_hx(0, 0, 128)
         load_sp(0, ((0, 64),))
         load_g(0)
         load_sp(0, ((64, 128),))
-        load_base(0, 128)
+        load_base(0)
         load_g(1)
         load_hx(1, 0, 128)
-        load_sc(128, 512)
+        load_sc(1)
+        load_base(1)
         load_sp(1, ((0, 128),))
         load_hx(0, 128, 512)
-        load_base(128, 512)
         load_sp(2, ((0, 128),))
         load_hx(1, 128, 512)
+        load_base(2)
+        load_base(3)
 
         gq = [kt([P, 1024], U32, "gq%d" % v) for v in range(4)]
         gs = [kt([P, 1024], U8, "gs%d" % v) for v in range(4)]
@@ -179,7 +187,7 @@ def tile_refiner_pa_v_kernel(tc, X, Y, Wx, bx, Wy, by, base_w, spline_w, spline_
                 S.copy(out=ggw[:, h * 512:(h + 1) * 512].rearrange("c (j p u) -> c j p u", j=2, u=2),
                        in_=pt[:].rearrange("c (j u p) -> c j p u", j=2, u=2))
             cols = slice(b * 512, (b + 1) * 512)
-            tiles = {}
+            tiles = {0: gg}
 
             def scaled(v):
                 def run():
@@ -191,29 +199,39 @@ def tile_refiner_pa_v_kernel(tc, X, Y, Wx, bx, Wy, by, base_w, spline_w, spline_
                 def run():
                     V.quantize_mx(out=gq[v][:, cols].bitcast(E5), scales=gs[v][:, cols], in_=tiles[v][:])
                 return run
-            for k, step in enumerate((scaled(0), scaled(1), quant(0), scaled(2), quant(1), scaled(3), quant(2), quant(3))):
+            for k, step in enumerate((quant(0), scaled(1), scaled(2), quant(1), scaled(3), quant(2), quant(3))):
                 task["gv%d.%d" % (b, k)] = step
 
         def base_task(it):
             def run():
                 isl = slice(it * P, (it + 1) * P)
                 t = wt([P, P, 4], BF16, "bg", 1)
-                S.copy(out=t[:], in_=base[:, :, isl].rearrange("p j w -> p w j"))
+                S.copy(out=t[:], in_=base[it][:].rearrange("p j w -> p w j"))
                 V.quantize_mx(out=bq[:, isl].bitcast(E4), scales=bs[:, isl], in_=t[:].rearrange("p w j -> p (w j)"))
             return run
 
         def w2_tasks(it):
+            mixed = {}
             tiles = {}
 
-            def product(h, half):
+            def mix(half):
                 def run():
-                    raw = sp[it][:].rearrange("p (j q k) -> p q k j", j=4, k=8)
-                    fac = sc[:, :, it * P:(it + 1) * P].rearrange("p j q -> p q j")
                     if half == 0:
-                        tiles[h] = grp()
-                    qs = slice(64 * half, 64 * half + 64)
-                    V.tensor_tensor(out=tiles[h][:].rearrange("p (k q j) -> p q k j", k=4, j=4)[:, qs],
-                                    in0=raw[:, qs, 4 * h:4 * h + 4], in1=fac[:, qs].unsqueeze(2).to_broadcast([P, 64, 4, 4]), op=ALU.mult)
+                        mixed["f"] = wt([P, P, 4], BF16, "sci", 2)
+                        V.tensor_copy(out=mixed["f"][:], in_=sc[it][:].rearrange("p j q -> p q j"))
+                    mixed[half] = wt([P, 2048], BF16, "mix", 2)
+                    src = sp[it][:].rearrange("p (j c) -> p c j", j=4)
+                    V.tensor_copy(out=mixed[half][:].rearrange("p (c j) -> p c j", j=4), in_=src[:, half * 512:(half + 1) * 512])
+                return run
+
+            def product(h):
+                def run():
+                    tiles[h] = grp()
+                    for half in range(2):
+                        qs = slice(64 * half, 64 * half + 64)
+                        V.tensor_tensor(out=tiles[h][:].rearrange("p (k q j) -> p k q j", k=4, j=4)[:, :, qs],
+                                        in0=mixed[half][:].rearrange("p (q k j) -> p k q j", k=8, j=4)[:, 4 * h:4 * h + 4],
+                                        in1=mixed["f"][:, qs].unsqueeze(1).to_broadcast([P, 4, 64, 4]), op=ALU.mult)
                 return run
 
             def quant(h):
@@ -221,7 +239,7 @@ def tile_refiner_pa_v_kernel(tc, X, Y, Wx, bx, Wy, by, base_w, spline_w, spline_
                     cols = slice(h * 512, (h + 1) * 512)
                     V.quantize_mx(out=wq[it][:, cols].bitcast(E4), scales=ws[it][:, cols], in_=tiles[h][:])
                 return run
-            for k, step in enumerate((product(0, 0), product(0, 1), product(1, 0), quant(0), product(1, 1), quant(1))):
+            for k, step in enumerate((mix(0), mix(1), product(0), quant(0), product(1), quant(1))):
                 task["w%d.%d" % (it, k)] = step
 
         for it in range(4):
@@ -247,7 +265,7 @@ def tile_refiner_pa_v_kernel(tc, X, Y, Wx, bx, Wy, by, base_w, spline_w, spline_
 
             def act(name, func, scale, bias=0.0):
                 def run():
-                    w[name] = wt([P, 512], F32, "w" + name, 2)
+                    w[name] = wt([P, 512], F32, "w", WGTS)
                     S.activation(w[name][:], h[:], func, bias=bias, scale=scale)
                 return run
 
@@ -260,9 +278,10 @@ def tile_refiner_pa_v_kernel(tc, X, Y, Wx, bx, Wy, by, base_w, spline_w, spline_
                     S.activation(w[name][:], w[name][:], ACT.Square, scale=math.sqrt(2.5))
                 return run
 
-            steps = [act("T", ACT.Tanh, -0.5), act("U", ACT.Silu, -1.0)]
-            for name in ("L2", "R2", "L3", "R3", "L1", "R1", "L4", "R4"):
-                steps += [relu(name), square(name)]
+            steps = [act("T", ACT.Tanh, 0.5), act("U", ACT.Silu, -1.0)]
+            for name, before in zip(KNOTS + (None, ), (None, ) + KNOTS):
+                steps += [relu(name)] if name else []
+                steps += [square(before)] if before else []
             for k, s in enumerate(steps):
                 task["f%d" % k] = s
             d = {}
@@ -301,18 +320,18 @@ def tile_refiner_pa_v_kernel(tc, X, Y, Wx, bx, Wy, by, base_w, spline_w, spline_
 
         sums = {}
 
-        def sum_transposes(n):
+        def sum_transposes(n, js=(0, 1, 2, 3)):
             sm = bank("sum")
-            for j in range(4):
-                js = slice(j * P, (j + 1) * P)
+            for k, j in enumerate(js):
                 for r in range(NT):
-                    T.matmul(sm[:, js], lhsT=prod[n, r][:, js], rhs=ident[:], is_transpose=True, start=(r == 0), stop=(r == NT - 1))
-            sums[n] = sm
+                    T.matmul(sm[:, k * P:(k + 1) * P], lhsT=prod[n, r][:, j * P:(j + 1) * P], rhs=ident[:], is_transpose=True, start=(r == 0), stop=(r == NT - 1))
+            sums[n, js[0]] = sm
 
-        def dz_final(n):
+        def dz_final(n, js=(0, 1, 2, 3)):
             it, b = ORDER[n]
-            V.scalar_tensor_tensor(out=dz[b][:, it * P:(it + 1) * P, :], in0=sqs[n][:].rearrange("p j q -> p q j"), scalar=0.5,
-                                   in1=sums[n][:].rearrange("p (j q) -> p q j", j=4), op0=ALU.subtract, op1=ALU.mult)
+            a, w = js[0], len(js)
+            V.scalar_tensor_tensor(out=dz[b][:, it * P:(it + 1) * P, a:a + w], in0=sqs[n][:, a:a + w].rearrange("p j q -> p q j"), scalar=0.5,
+                                   in1=sums[n, a][:, 0:w * P].rearrange("p (j q) -> p q j", j=w), op0=ALU.subtract, op1=ALU.mult)
 
         def dz_quant(n):
             it, b = ORDER[n]
@@ -321,21 +340,22 @@ def tile_refiner_pa_v_kernel(tc, X, Y, Wx, bx, Wy, by, base_w, spline_w, spline_
 
         dzt = {}
 
-        def dz2(b):
+        def dz2(b, v):
             def run():
                 words = dz[b][:].rearrange("p i j -> p (i j)").bitcast(F32)
-                dzt[b] = grp()
-                for v in range(2):
-                    pt = bank("misc")
-                    for t in range(4):
-                        T.transpose(pt[:, t * P:(t + 1) * P], words[:, 2 * t + v::8], ident[:])
-                    copy(ENG["dz2.%d" % b][v], dzt[b][:, v * 1024:(v + 1) * 1024].rearrange("c (e p t) -> c e p t", e=2, t=4),
-                         pt[:].bitcast(BF16).rearrange("c (t p e) -> c e p t", t=4, e=2))
+                if v == 0:
+                    dzt[b] = grp()
+                pt = bank("misc")
+                for t in range(4):
+                    T.transpose(pt[:, t * P:(t + 1) * P], words[:, 2 * t + v::8], ident[:])
+                copy(ENG["dz2.%d" % b][v], dzt[b][:, v * 1024:(v + 1) * 1024].rearrange("c (e p t) -> c e p t", e=2, t=4),
+                     pt[:].bitcast(BF16).rearrange("c (t p e) -> c e p t", t=4, e=2))
             return run
 
-        def dz2_quant(b):
+        def dz2_quant(b, v):
             def run():
-                V.quantize_mx(out=eq[b][:].bitcast(E5), scales=es[b][:], in_=dzt[b][:])
+                cols = slice(v * 256, (v + 1) * 256)
+                V.quantize_mx(out=eq[b][:, cols].bitcast(E5), scales=es[b][:, cols], in_=dzt[b][:, v * 1024:(v + 1) * 1024])
             return run
 
         raws = {}
@@ -396,21 +416,23 @@ def tile_refiner_pa_v_kernel(tc, X, Y, Wx, bx, Wy, by, base_w, spline_w, spline_
                 nc.sync.dma_start(out=out_0[b, h * 64:(h + 1) * 64].rearrange("t (p j) f -> p t (j f)", j=4), in_=o[:].rearrange("p (t r) -> p t r", r=32))
             return run
 
-        def out0_flat(b):
-            flat = []
-            for j in range(4):
-                if j % 2 == 0:
-                    o = stage()[:].bitcast(F32)
-                oj = o[:, (j % 2) * 1024:(j % 2 + 1) * 1024].rearrange("p (f t) -> p f t", f=8)
+        flat = {}
+
+        def out0_flat(b, j):
+            def run():
+                o = wt([P, 2048], BF16, "mix", 2) if j < 2 else grp()
+                flat[j] = o[:].bitcast(F32).rearrange("p (f t) -> p f t", f=8)
                 for h in range(2):
                     pt = out0_matmul(b, j, h, "misc" if h else "da")
-                    copy("v" if h else "s", oj[:, :, h * 64:(h + 1) * 64], pt[:].rearrange("p (t f) -> p f t", f=8))
-                flat.append(oj)
-            return flat
+                    copy("v" if h else "s", flat[j][:, :, h * 64:(h + 1) * 64], pt[:].rearrange("p (t f) -> p f t", f=8))
+            return run
 
-        def out0_by_t(b, flat):
-            halves = [stage()[:].bitcast(F32).rearrange("t (p j f) -> t p j f", j=4, f=8) for half in range(2)]
-            for j in range(4):
+        halves = []
+
+        def out0_turn(b, j):
+            def run():
+                if j == 0:
+                    halves.extend(stage()[:].bitcast(F32).rearrange("t (p j f) -> t p j f", j=4, f=8) for half in range(2))
                 for g in range(2):
                     pt = bank("misc" if g else "da")
                     for f in range(4):
@@ -418,6 +440,9 @@ def tile_refiner_pa_v_kernel(tc, X, Y, Wx, bx, Wy, by, base_w, spline_w, spline_
                     src = pt[:].rearrange("t (f p) -> t p f", f=4)
                     for half in range(2):
                         copy("v" if g else "s", halves[half][:, :, j, 4 * g:4 * g + 4], src[:, half * 64:(half + 1) * 64])
+            return run
+
+        def out0_store(b):
             for half in range(2):
                 nc.sync.dma_start(out=out_0[b, :, half * 256:(half + 1) * 256, :].rearrange("t (p j) f -> t p j f", j=4), in_=halves[half])
 
@@ -429,8 +454,9 @@ def tile_refiner_pa_v_kernel(tc, X, Y, Wx, bx, Wy, by, base_w, spline_w, spline_
             for h in range(2):
                 task["x%d.%d" % (b, h)] = x_copy(b, h)
                 task["xq%d.%d" % (b, h)] = x_quant(b, h)
-            task["dz2.%d" % b] = dz2(b)
-            task["dz2q.%d" % b] = dz2_quant(b)
+            for v in range(2):
+                task["dz2.%d%d" % (b, v)] = dz2(b, v)
+                task["dz2q.%d%d" % (b, v)] = dz2_quant(b, v)
         for it in range(4):
             task["out1.%d" % it] = out1(it)
 
@@ -444,8 +470,10 @@ def tile_refiner_pa_v_kernel(tc, X, Y, Wx, bx, Wy, by, base_w, spline_w, spline_
         for n in range(len(ORDER)):
             d = weights(n + 1) if n + 1 < len(ORDER) else {}
             if n == 1:
+                load_sc(2)
                 load_sp(3, ((0, 128),))
             elif n == 2:
+                load_sc(3)
                 raws["x0"] = load_x(0)
             elif n == 3:
                 raws["x1"] = load_x(1)
@@ -472,11 +500,13 @@ def tile_refiner_pa_v_kernel(tc, X, Y, Wx, bx, Wy, by, base_w, spline_w, spline_
                 if n > 0 and r == SUM_AT + 2:
                     dz_quant(n - 1)
 
-        task["sum"] = lambda: sum_transposes(7)
-        task["fin"] = lambda: dz_final(7)
+        for a in (0, 2):
+            task["sum%d" % a] = lambda a=a: sum_transposes(7, (a, a + 1))
+            task["fin%d" % a] = lambda a=a: dz_final(7, (a, a + 1))
         task["dzq"] = lambda: dz_quant(7)
-        flat = []
-        task["o0mm"] = lambda: flat.extend(out0_flat(1))
-        task["o0tr"] = lambda: out0_by_t(1, flat)
+        for j in range(4):
+            task["mm%d" % j] = out0_flat(1, j)
+            task["tr%d" % j] = out0_turn(1, j)
+        task["store"] = lambda: out0_store(1)
         for name in TAIL:
             task[name]()

@@ -46,22 +46,21 @@ TERMS = (
 NT = len(TERMS)
 PRODS = 16
 WGTS = 14
-KNOTS = ("L2", "R2", "L3", "R3", "L1", "R1", "L4", "R4")
 ORDER = ((0, 0), (0, 1), (1, 0), (2, 0), (1, 1), (3, 0), (2, 1), (3, 1))
 PLAN = {
-    0: ((0, "w1.0"), (0, "gv1.1"), (0, "gv1.0"), (1, "gv1.4"), (1, "base1"), (2, "gv1.6"), (2, "gv1.2"), (3, "gv1.3"), (6, "w1.1"), (6, "w1.2"), (6, "base2"), (7, "gv1.5"), (8, "w1.3")),
-    1: ((2, "w1.4"), (3, "w2.0"), (4, "w1.5"), (4, "base3"), (7, "w2.1")),
-    2: ((0, "w2.2"), (1, "w2.4"), (1, "w3.0"), (3, "w2.5"), (4, "w2.3")),
-    3: ((1, "x0.0"), (1, "w3.1"), (3, "w3.2")),
-    4: ((0, "w3.4"), (3, "x0.1"), (3, "w3.5"), (4, "w3.3")),
-    5: ((0, "x1.0"), (0, "x1.1"), (3, "xq1.0"), (4, "xq0.0"), (6, "xq0.1"), (6, "xq1.1")),
-    6: ((1, "out1.0"), (7, "out1.1")),
-    7: ((1, "dz2.00"), (1, "dz2.01"), (1, "dz2q.01"), (1, "wx.1"), (2, "wx.0"), (4, "dz2q.00"), (4, "wx.3"), (4, "wx.2"), (5, "out0.1"), (8, "out0.0")),
+    0: ((0, "w1.0"), (0, "w1.1"), (0, "gv1.1"), (1, "w1.2"), (1, "gv1.0"), (2, "gv1.2"), (2, "base1"), (3, "gv1.5"), (3, "w1.4"), (4, "gv1.4"), (6, "gv1.6"), (6, "gv1.3")),
+    1: ((1, "w1.3"), (1, "w2.0"), (2, "w2.1"), (3, "base2"), (4, "w1.5")),
+    2: ((0, "w2.2"), (0, "w2.4"), (3, "base3"), (4, "w3.0"), (4, "w3.1"), (6, "w2.3"), (7, "w2.5")),
+    3: ((0, "w3.2"), (1, "w3.4"), (4, "w3.3")),
+    4: ((2, "x0.0"), (3, "w3.5"), (4, "x0.1")),
+    5: ((0, "xq0.0"), (1, "x1.1"), (1, "xq1.1"), (3, "x1.0"), (4, "xq0.1")),
+    6: ((0, "xq1.0"), (2, "wx.0"), (2, "wx.1"), (4, "out1.0"), (4, "wx.3"), (6, "out1.1")),
+    7: ((0, "dz2.00"), (0, "dz2q.00"), (0, "dz2.01"), (0, "dz2q.01"), (1, "wx.2"), (4, "out0.1"), (8, "out0.0")),
 }
-ENG = {"x": "v", "wx": "s", "out1.0": "vs", "out1.1": "vs", "out1.2": "ss", "out1.3": "vs", "dz2.0": "vv", "dz2.1": "vs", "out0.0": "svvv", "out0.1": "vsss"}
-WPOS = (0, 0, 1, 1, 1, 2, 3, 3, 3, 3, 4, 4, 5, 6, 6, 8, 8, 8)
-PROLOGUE = ("w0.0", "hx0", "f0", "w0.1", "f1", "g0", "gv0.2", "f2", "gv0.1", "f3", "w0.2", "f4", "gv0.3", "f5", "w0.4", "w0.3", "f6", "gv0.0", "f7", "f8", "f9", "gv0.4", "f10", "gv0.5", "base0", "w0.5", "f11", "f12", "hx1", "f13", "gv0.6", "f14", "g1", "f15", "f16", "f17")
-TAIL = ("sum0", "fin0", "dz2.10", "sum2", "fin2", "dz2.11", "dz2q.10", "mm0", "dz2q.11", "mm1", "mm2", "mm3", "tr0", "tr1", "tr2", "tr3", "store", "dzq", "out1.3", "out1.2")
+ENG = {"mix0": "vv", "mix1": "vv", "mix2": "vv", "mix3": "sv", "x": "vvsv", "wx": "vv", "out1.0": "vv", "out1.1": "vv", "out1.2": "vs", "out1.3": "ss", "dz2.0": "vv", "dz2.1": "ss", "out0.0": "ssvs", "out0.1": "ssss"}
+WPOS = (0, 0, 1, 2, 2, 2, 2, 3, 4, 4, 4, 4, 5, 5, 5, 6, 6, 7)
+PROLOGUE = ("hx0", "w0.0", "f0", "f1", "f2", "w0.1", "f3", "w0.2", "g0", "gv0.4", "gv0.0", "w0.4", "f4", "f5", "f6", "gv0.2", "w0.3", "gv0.5", "base0", "gv0.1", "f7", "f8", "f9", "gv0.6", "gv0.3", "w0.5", "f10", "hx1", "f11", "f12", "f13", "g1", "f14", "f15", "f16", "f17")
+TAIL = ("sum0", "fin0", "dz2.10", "dz2q.10", "sum2", "fin2", "mm0", "dz2.11", "mm1", "dz2q.11", "tr0", "mm2", "tr1", "mm3", "tr2", "tr3", "dzq", "store", "out1.2", "out1.3")
 
 
 def tile_refiner_pa_v_kernel(tc, X, Y, Wx, bx, Wy, by, base_w, spline_w, spline_scaler, Hx, grad_out, out_0, out_1):
@@ -221,7 +220,7 @@ def tile_refiner_pa_v_kernel(tc, X, Y, Wx, bx, Wy, by, base_w, spline_w, spline_
                         V.tensor_copy(out=mixed["f"][:], in_=sc[it][:].rearrange("p j q -> p q j"))
                     mixed[half] = wt([P, 2048], BF16, "mix", 2)
                     src = sp[it][:].rearrange("p (j c) -> p c j", j=4)
-                    V.tensor_copy(out=mixed[half][:].rearrange("p (c j) -> p c j", j=4), in_=src[:, half * 512:(half + 1) * 512])
+                    copy(ENG["mix%d" % it][half], mixed[half][:].rearrange("p (c j) -> p c j", j=4), src[:, half * 512:(half + 1) * 512])
                 return run
 
             def product(h):
@@ -279,7 +278,8 @@ def tile_refiner_pa_v_kernel(tc, X, Y, Wx, bx, Wy, by, base_w, spline_w, spline_
                 return run
 
             steps = [act("T", ACT.Tanh, 0.5), act("U", ACT.Silu, -1.0)]
-            for name, before in zip(KNOTS + (None, ), (None, ) + KNOTS):
+            knots = [t[0] for t in TERMS[1:]]
+            for name, before in zip(knots + [None], [None] + knots):
                 steps += [relu(name)] if name else []
                 steps += [square(before)] if before else []
             for k, s in enumerate(steps):
@@ -364,7 +364,7 @@ def tile_refiner_pa_v_kernel(tc, X, Y, Wx, bx, Wy, by, base_w, spline_w, spline_
         def wx_copy(h):
             def run():
                 wxt[h] = grp()
-                copy(ENG["wx"], wxt[h][:].rearrange("p (w j) -> p w j", j=4), raws["wx"][:].rearrange("p (j w) -> p w j", j=4)[:, h * 512:(h + 1) * 512, :])
+                copy(ENG["wx"][h], wxt[h][:].rearrange("p (w j) -> p w j", j=4), raws["wx"][:].rearrange("p (j w) -> p w j", j=4)[:, h * 512:(h + 1) * 512, :])
             return run
 
         def wx_quant(h):
@@ -377,7 +377,7 @@ def tile_refiner_pa_v_kernel(tc, X, Y, Wx, bx, Wy, by, base_w, spline_w, spline_
         def x_copy(b, h):
             def run():
                 xg[b, h] = grp()
-                copy(ENG["x"], xg[b, h][:].rearrange("p (t f j) -> p t f j", f=8, j=4),
+                copy(ENG["x"][2 * b + h], xg[b, h][:].rearrange("p (t f j) -> p t f j", f=8, j=4),
                      raws["x%d" % b][:].rearrange("p (t j f) -> p t f j", j=4, f=8)[:, h * 64:(h + 1) * 64])
             return run
 

from contextlib import ExitStack
import math

import concourse.mybir as mybir
from concourse.masks import make_identity

F32 = mybir.dt.float32
BF16 = mybir.dt.bfloat16
U32 = mybir.dt.uint32
U8 = mybir.dt.uint8
E4 = mybir.dt.float8_e4m3fn_x4
E5 = mybir.dt.float8_e5m2_x4
ALU = mybir.AluOpType
ACT = mybir.ActivationFunctionType
OPS = {"add": ALU.add, "mult": ALU.mult}

FLOPS = 2 * 1024 * 512 * 4608 + 2 * 2 * 1024 * 512 * 1024
BYTES = 2 * (1048576 + 524288 + 262144 + 2097152 + 262144 + 524288) + 4 * (524288 + 1048576 + 524288)

P = 128
SUM_AT = 4
POS, NEG4, POS4, POS2 = 0, 1, 2, 3
VARIANT = (1.0, -4.0, 4.0, 2.0)
CHAIN = ((POS,), (NEG4,), (POS4, POS2), (NEG4,))


def left(j):
    return tuple((1 + k, v) for k in range(j - 1, 4) for v in CHAIN[k + 1 - j])


def right(j):
    return tuple((1 + k, v) for k in range(7, 3, -1) if 0 <= j - (k - 3) for v in CHAIN[j - (k - 3)])


TERMS = (
    ("T", "add", 1.0, ((0, POS),)),
    ("L2", "mult", 1.0, left(2)),
    ("R2", "mult", -1.0, right(2)),
    ("L3", "mult", 1.0, left(3)),
    ("R3", "mult", -1.0, right(3)),
    ("L1", "mult", 1.0, left(1)),
    ("R1", "mult", -1.0, right(1)),
    ("L4", "mult", 1.0, left(4)),
    ("R4", "mult", -1.0, right(4)),
)
NT = len(TERMS)
PRODS = 16
WGTS = 14
ORDER = ((0, 0), (0, 1), (1, 0), (2, 0), (1, 1), (3, 0), (2, 1), (3, 1))
PLAN = {
    0: ((0, "w1.0"), (0, "w1.1"), (0, "gv1.1"), (1, "w1.2"), (1, "gv1.0"), (2, "gv1.2"), (2, "base1"), (3, "gv1.5"), (3, "w1.4"), (4, "gv1.4"), (6, "gv1.6"), (6, "gv1.3")),
    1: ((1, "w1.3"), (1, "w2.0"), (2, "w2.1"), (3, "base2"), (4, "w1.5")),
    2: ((0, "w2.2"), (0, "w2.4"), (3, "base3"), (4, "w3.0"), (4, "w3.1"), (6, "w2.3"), (7, "w2.5")),
    3: ((0, "w3.2"), (1, "w3.4"), (4, "w3.3")),
    4: ((2, "x0.0"), (3, "w3.5"), (4, "x0.1")),
    5: ((0, "xq0.0"), (1, "x1.1"), (1, "xq1.1"), (3, "x1.0"), (4, "xq0.1")),
    6: ((0, "xq1.0"), (2, "wx.0"), (2, "wx.1"), (4, "out1.0"), (4, "wx.3"), (6, "out1.1")),
    7: ((0, "dz2.00"), (0, "dz2q.00"), (0, "dz2.01"), (0, "dz2q.01"), (1, "wx.2"), (4, "out0.1"), (8, "out0.0")),
}
ENG = {"mix0": "vv", "mix1": "vv", "mix2": "vv", "mix3": "sv", "x": "vvsv", "wx": "vv", "out1.0": "vv", "out1.1": "vv", "out1.2": "vs", "out1.3": "ss", "dz2.0": "vv", "dz2.1": "ss", "out0.0": "ssvs", "out0.1": "ssss"}
WPOS = (0, 0, 1, 2, 2, 2, 2, 3, 4, 4, 4, 4, 5, 5, 5, 6, 6, 7)
PROLOGUE = ("hx0", "w0.0", "f0", "f1", "f2", "w0.1", "f3", "w0.2", "g0", "gv0.4", "gv0.0", "w0.4", "f4", "f5", "f6", "gv0.2", "w0.3", "gv0.5", "base0", "gv0.1", "f7", "f8", "f9", "gv0.6", "gv0.3", "w0.5", "f10", "hx1", "f11", "f12", "f13", "g1", "f14", "f15", "f16", "f17")
TAIL = ("sum0", "fin0", "dz2.10", "dz2q.10", "sum2", "fin2", "mm0", "dz2.11", "mm1", "dz2q.11", "tr0", "mm2", "tr1", "mm3", "tr2", "tr3", "dzq", "store", "out1.2", "out1.3")


def tile_refiner_pa_v_kernel(tc, X, Y, Wx, bx, Wy, by, base_w, spline_w, spline_scaler, Hx, grad_out, out_0, out_1):
    nc = tc.nc
    V, S, T = nc.vector, nc.scalar, nc.tensor
    with ExitStack() as ctx:
        keep = ctx.enter_context(tc.tile_pool(name="keep", bufs=1))
        work = ctx.enter_context(tc.tile_pool(name="work", bufs=1))
        psum = ctx.enter_context(tc.psum_pool(name="psum", bufs=1))
        ctx.enter_context(tc.manual_schedule())

        def kt(shape, dt, name):
            return keep.tile(shape, dt, name=name, tag=name, align_bytes=64)

        def wt(shape, dt, tag, bufs):
            return work.tile(shape, dt, name=tag, tag=tag, bufs=bufs, align_bytes=64)

        def bank(tag):
            return psum.tile([P, 512], F32, name=tag, tag=tag, bufs={"da": 4, "sum": 2, "misc": 2}[tag])

        def stage():
            return wt([P, 4096], BF16, "stage", 3)

        def grp():
            return wt([P, 2048], BF16, "grp", 4)

        def copy(engine, out, in_):
            if engine == "v":
                V.tensor_copy(out=out, in_=in_)
            else:
                S.copy(out=out, in_=in_)

        ident = kt([P, P], F32, "ident")
        warm = kt([P, 1], F32, "warm")
        V.memset(warm[:], 0.0)
        S.activation(warm[:], warm[:], ACT.Silu)
        make_identity(nc, ident[:])

        g_raw = stage()
        hx = [kt([P, 4, 512], F32, "hx%d" % b) for b in range(2)]
        sc = {}
        base = {}
        sp = {}

        def load_g(b):
            nc.sync.dma_start(out=g_raw[:, b * 2048:(b + 1) * 2048].rearrange("p (j o) -> p j o", j=4),
                              in_=grad_out[b].rearrange("(p j) o -> p j o", j=4))

        def load_hx(b, c0, c1):
            nc.sync.dma_start(out=hx[b][:, :, c0:c1], in_=Hx[b * 512:(b + 1) * 512, c0:c1].rearrange("(p j) i -> p j i", j=4))

        def load_rows(name, store, it, src):
            store[it] = wt([P, 4, P], BF16, name, 4 if name == "base" else 2)
            nc.sync.dma_start(out=store[it][:], in_=src[:, it * P:(it + 1) * P].rearrange("(p j) i -> p j i", j=4))

        def load_sc(it):
            load_rows("sc", sc, it, spline_scaler)

        def load_base(it):
            load_rows("base", base, it, base_w)

        def load_sp(it, pieces):
            if it not in sp:
                sp[it] = stage()
            for c0, c1 in pieces:
                nc.sync.dma_start(out=sp[it][:].rearrange("p (j w) -> p j w", j=4)[:, :, 8 * c0:8 * c1],
                                  in_=spline_w[:, it * P + c0:it * P + c1, :].rearrange("(p j) i k -> p j (i k)", j=4))

        def load_x(b):
            t = stage()
            nc.sync.dma_start(out=t[:].rearrange("p (t r) -> p t r", r=32), in_=X[b].rearrange("t (p j) f -> p t (j f)", j=4))
            return t

        def load_wx():
            t = stage()
            nc.sync.dma_start(out=t[:].rearrange("p (j w) -> p j w", j=4), in_=Wx.rearrange("(p j) w -> p j w", j=4))
            return t

        load_sc(0)
        load_hx(0, 0, 128)
        load_sp(0, ((0, 64),))
        load_g(0)
        load_sp(0, ((64, 128),))
        load_base(0)
        load_g(1)
        load_hx(1, 0, 128)
        load_sc(1)
        load_base(1)
        load_sp(1, ((0, 128),))
        load_hx(0, 128, 512)
        load_sp(2, ((0, 128),))
        load_hx(1, 128, 512)
        load_base(2)
        load_base(3)

        gq = [kt([P, 1024], U32, "gq%d" % v) for v in range(4)]
        gs = [kt([P, 1024], U8, "gs%d" % v) for v in range(4)]
        bq = kt([P, 512], U32, "bq")
        bs = kt([P, 512], U8, "bs")
        wq = [kt([P, 1024], U32, "wq%d" % it) for it in range(4)]
        ws = [kt([P, 1024], U8, "ws%d" % it) for it in range(4)]
        dq = [kt([P, 512], U32, "dq%d" % b) for b in range(2)]
        ds = [kt([P, 512], U8, "ds%d" % b) for b in range(2)]
        eq = [kt([P, 512], U32, "eq%d" % b) for b in range(2)]
        es = [kt([P, 512], U8, "es%d" % b) for b in range(2)]
        xq = [kt([P, 1024], U32, "xq%d" % b) for b in range(2)]
        xs = [kt([P, 1024], U8, "xs%d" % b) for b in range(2)]
        vq = kt([P, 1024], U32, "vq")
        vs = kt([P, 1024], U8, "vs")
        dz = [kt([P, 512, 4], BF16, "dz%d" % b) for b in range(2)]
        task = {}

        def g_transposes(b):
            words = g_raw[:].bitcast(F32)
            gg = wt([P, 2048], BF16, "gg", 1)
            ggw = gg[:].bitcast(F32)
            for h in range(2):
                pt = bank("misc")
                for jj in range(2):
                    for u in range(2):
                        w0 = (b * 4 + 2 * h + jj) * 256
                        T.transpose(pt[:, (2 * jj + u) * P:(2 * jj + u + 1) * P], words[:, w0 + u:w0 + 256:2], ident[:])
                S.copy(out=ggw[:, h * 512:(h + 1) * 512].rearrange("c (j p u) -> c j p u", j=2, u=2),
                       in_=pt[:].rearrange("c (j u p) -> c j p u", j=2, u=2))
            cols = slice(b * 512, (b + 1) * 512)
            tiles = {0: gg}

            def scaled(v):
                def run():
                    tiles[v] = grp()
                    V.tensor_scalar(out=tiles[v][:], in0=gg[:], scalar1=VARIANT[v], scalar2=None, op0=ALU.mult)
                return run

            def quant(v):
                def run():
                    V.quantize_mx(out=gq[v][:, cols].bitcast(E5), scales=gs[v][:, cols], in_=tiles[v][:])
                return run
            for k, step in enumerate((quant(0), scaled(1), scaled(2), quant(1), scaled(3), quant(2), quant(3))):
                task["gv%d.%d" % (b, k)] = step

        def base_task(it):
            def run():
                isl = slice(it * P, (it + 1) * P)
                t = wt([P, P, 4], BF16, "bg", 1)
                S.copy(out=t[:], in_=base[it][:].rearrange("p j w -> p w j"))
                V.quantize_mx(out=bq[:, isl].bitcast(E4), scales=bs[:, isl], in_=t[:].rearrange("p w j -> p (w j)"))
            return run

        def w2_tasks(it):
            mixed = {}
            tiles = {}

            def mix(half):
                def run():
                    if half == 0:
                        mixed["f"] = wt([P, P, 4], BF16, "sci", 2)
                        V.tensor_copy(out=mixed["f"][:], in_=sc[it][:].rearrange("p j q -> p q j"))
                    mixed[half] = wt([P, 2048], BF16, "mix", 2)
                    src = sp[it][:].rearrange("p (j c) -> p c j", j=4)
                    copy(ENG["mix%d" % it][half], mixed[half][:].rearrange("p (c j) -> p c j", j=4), src[:, half * 512:(half + 1) * 512])
                return run

            def product(h):
                def run():
                    tiles[h] = grp()
                    for half in range(2):
                        qs = slice(64 * half, 64 * half + 64)
                        V.tensor_tensor(out=tiles[h][:].rearrange("p (k q j) -> p k q j", k=4, j=4)[:, :, qs],
                                        in0=mixed[half][:].rearrange("p (q k j) -> p k q j", k=8, j=4)[:, 4 * h:4 * h + 4],
                                        in1=mixed["f"][:, qs].unsqueeze(1).to_broadcast([P, 4, 64, 4]), op=ALU.mult)
                return run

            def quant(h):
                def run():
                    cols = slice(h * 512, (h + 1) * 512)
                    V.quantize_mx(out=wq[it][:, cols].bitcast(E4), scales=ws[it][:, cols], in_=tiles[h][:])
                return run
            for k, step in enumerate((mix(0), mix(1), product(0), quant(0), product(1), quant(1))):
                task["w%d.%d" % (it, k)] = step

        for it in range(4):
            task["base%d" % it] = base_task(it)
            w2_tasks(it)

        ht = {}

        def hx_transposes(n):
            it, b = ORDER[n]
            pt = bank("misc")
            for j in range(4):
                T.transpose(pt[:, j * P:(j + 1) * P], hx[b][:, j, it * P:(it + 1) * P], ident[:])
            ht[n] = wt([P, 512], F32, "ht", 2)
            S.copy(out=ht[n][:], in_=pt[:])

        wgt = {}

        def weights(n):
            h = ht[n]
            w = {}
            wgt[n] = w

            def act(name, func, scale, bias=0.0):
                def run():
                    w[name] = wt([P, 512], F32, "w", WGTS)
                    S.activation(w[name][:], h[:], func, bias=bias, scale=scale)
                return run

            def relu(name):
                sign = 1.0 if name[0] == "R" else -1.0
                return act(name, ACT.Relu, sign * 2.5, sign * (2.5 - int(name[1])))

            def square(name):
                def run():
                    S.activation(w[name][:], w[name][:], ACT.Square, scale=math.sqrt(2.5))
                return run

            steps = [act("T", ACT.Tanh, 0.5), act("U", ACT.Silu, -1.0)]
            knots = [t[0] for t in TERMS[1:]]
            for name, before in zip(knots + [None], [None] + knots):
                steps += [relu(name)] if name else []
                steps += [square(before)] if before else []
            for k, s in enumerate(steps):
                task["f%d" % k] = s
            d = {}
            for k, s in zip(WPOS, steps):
                d.setdefault(k, []).append(s)
            return d

        sqs = {}

        def hx_square(n):
            it, b = ORDER[n]
            sqs[n] = wt([P, 4, P], F32, "sq", 2)
            S.activation(sqs[n][:], hx[b][:, :, it * P:(it + 1) * P], ACT.Square, scale=math.sqrt(0.5))

        prod = {}

        def term(n, r):
            it, b = ORDER[n]
            name, op, const, passes = TERMS[r]
            da = bank("da")
            cols = slice(b * 512, (b + 1) * 512)
            for s, (c, v) in enumerate(passes):
                if c == 0:
                    lq, ls = bq[:, it * P:(it + 1) * P], bs[:, it * P:(it + 1) * P]
                else:
                    lq, ls = wq[it][:, (c - 1) * P:c * P], ws[it][:, (c - 1) * P:c * P]
                T.matmul_mx(out=da[:], lhsT=lq.bitcast(E4), lhsT_scale=ls, rhs=gq[v][:, cols].bitcast(E5), rhs_scale=gs[v][:, cols],
                            start=(s == 0), stop=(s == len(passes) - 1))
            pr = wt([P, 512], F32, "prod", PRODS)
            V.scalar_tensor_tensor(out=pr[:], in0=wgt[n][name][:], scalar=const, in1=da[:], op0=OPS[op], op1=ALU.mult)
            prod[n, r] = pr

        def silu_second(n):
            pr = prod[n, 0]
            V.scalar_tensor_tensor(out=pr[:], in0=wgt[n]["U"][:], scalar=1.0, in1=pr[:], op0=ALU.subtract, op1=ALU.mult)

        sums = {}

        def sum_transposes(n, js=(0, 1, 2, 3)):
            sm = bank("sum")
            for k, j in enumerate(js):
                for r in range(NT):
                    T.matmul(sm[:, k * P:(k + 1) * P], lhsT=prod[n, r][:, j * P:(j + 1) * P], rhs=ident[:], is_transpose=True, start=(r == 0), stop=(r == NT - 1))
            sums[n, js[0]] = sm

        def dz_final(n, js=(0, 1, 2, 3)):
            it, b = ORDER[n]
            a, w = js[0], len(js)
            V.scalar_tensor_tensor(out=dz[b][:, it * P:(it + 1) * P, a:a + w], in0=sqs[n][:, a:a + w].rearrange("p j q -> p q j"), scalar=0.5,
                                   in1=sums[n, a][:, 0:w * P].rearrange("p (j q) -> p q j", j=w), op0=ALU.subtract, op1=ALU.mult)

        def dz_quant(n):
            it, b = ORDER[n]
            isl = slice(it * P, (it + 1) * P)
            V.quantize_mx(out=dq[b][:, isl].bitcast(E5), scales=ds[b][:, isl], in_=dz[b][:, isl, :].rearrange("p q j -> p (q j)"))

        dzt = {}

        def dz2(b, v):
            def run():
                words = dz[b][:].rearrange("p i j -> p (i j)").bitcast(F32)
                if v == 0:
                    dzt[b] = grp()
                pt = bank("misc")
                for t in range(4):
                    T.transpose(pt[:, t * P:(t + 1) * P], words[:, 2 * t + v::8], ident[:])
                copy(ENG["dz2.%d" % b][v], dzt[b][:, v * 1024:(v + 1) * 1024].rearrange("c (e p t) -> c e p t", e=2, t=4),
                     pt[:].bitcast(BF16).rearrange("c (t p e) -> c e p t", t=4, e=2))
            return run

        def dz2_quant(b, v):
            def run():
                cols = slice(v * 256, (v + 1) * 256)
                V.quantize_mx(out=eq[b][:, cols].bitcast(E5), scales=es[b][:, cols], in_=dzt[b][:, v * 1024:(v + 1) * 1024])
            return run

        raws = {}
        wxt = {}

        def wx_copy(h):
            def run():
                wxt[h] = grp()
                copy(ENG["wx"][h], wxt[h][:].rearrange("p (w j) -> p w j", j=4), raws["wx"][:].rearrange("p (j w) -> p w j", j=4)[:, h * 512:(h + 1) * 512, :])
            return run

        def wx_quant(h):
            def run():
                V.quantize_mx(out=vq[:, h * 512:(h + 1) * 512].bitcast(E4), scales=vs[:, h * 512:(h + 1) * 512], in_=wxt[h][:])
            return run

        xg = {}

        def x_copy(b, h):
            def run():
                xg[b, h] = grp()
                copy(ENG["x"][2 * b + h], xg[b, h][:].rearrange("p (t f j) -> p t f j", f=8, j=4),
                     raws["x%d" % b][:].rearrange("p (t j f) -> p t f j", j=4, f=8)[:, h * 64:(h + 1) * 64])
            return run

        def x_quant(b, h):
            def run():
                cols = slice(h * 512, (h + 1) * 512)
                V.quantize_mx(out=xq[b][:, cols].bitcast(E4), scales=xs[b][:, cols], in_=xg[b, h][:])
            return run

        def out1(it):
            def run():
                o = wt([P, 2048], F32, "ot", 2)
                for h in range(2):
                    pt = bank("misc")
                    for b in range(2):
                        T.matmul_mx(out=pt[:], lhsT=dq[b][:, it * P:(it + 1) * P].bitcast(E5), lhsT_scale=ds[b][:, it * P:(it + 1) * P],
                                    rhs=xq[b][:, h * 512:(h + 1) * 512].bitcast(E4), rhs_scale=xs[b][:, h * 512:(h + 1) * 512],
                                    start=(b == 0), stop=(b == 1))
                    copy(ENG["out1.%d" % it][h], o[:, h * 512:(h + 1) * 512], pt[:])
                nc.sync.dma_start(out=out_1[it * P:(it + 1) * P, :], in_=o[:, 0:1024])
            return run

        def out0_matmul(b, j, h, tag):
            pt = bank(tag)
            T.matmul_mx(out=pt[:], lhsT=eq[b][:, j * P:(j + 1) * P].bitcast(E5), lhsT_scale=es[b][:, j * P:(j + 1) * P],
                        rhs=vq[:, h * 512:(h + 1) * 512].bitcast(E4), rhs_scale=vs[:, h * 512:(h + 1) * 512], start=True, stop=True)
            return pt

        def out0(b, h):
            def run():
                o = wt([P, 2048], F32, "ot", 2)
                ov = o[:].rearrange("p (t j f) -> p t j f", j=4, f=8)
                for j in range(4):
                    pt = out0_matmul(b, j, h, "misc")
                    copy(ENG["out0.%d" % h][j], ov[:, :, j, :], pt[:].rearrange("p (t f) -> p t f", f=8))
                nc.sync.dma_start(out=out_0[b, h * 64:(h + 1) * 64].rearrange("t (p j) f -> p t (j f)", j=4), in_=o[:].rearrange("p (t r) -> p t r", r=32))
            return run

        flat = {}

        def out0_flat(b, j):
            def run():
                o = wt([P, 2048], BF16, "mix", 2) if j < 2 else grp()
                flat[j] = o[:].bitcast(F32).rearrange("p (f t) -> p f t", f=8)
                for h in range(2):
                    pt = out0_matmul(b, j, h, "misc" if h else "da")
                    copy("v" if h else "s", flat[j][:, :, h * 64:(h + 1) * 64], pt[:].rearrange("p (t f) -> p f t", f=8))
            return run

        halves = []

        def out0_turn(b, j):
            def run():
                if j == 0:
                    halves.extend(stage()[:].bitcast(F32).rearrange("t (p j f) -> t p j f", j=4, f=8) for half in range(2))
                for g in range(2):
                    pt = bank("misc" if g else "da")
                    for f in range(4):
                        T.transpose(pt[:, f * P:(f + 1) * P], flat[j][:, 4 * g + f, :], ident[:])
                    src = pt[:].rearrange("t (f p) -> t p f", f=4)
                    for half in range(2):
                        copy("v" if g else "s", halves[half][:, :, j, 4 * g:4 * g + 4], src[:, half * 64:(half + 1) * 64])
            return run

        def out0_store(b):
            for half in range(2):
                nc.sync.dma_start(out=out_0[b, :, half * 256:(half + 1) * 256, :].rearrange("t (p j) f -> t p j f", j=4), in_=halves[half])

        for h in range(2):
            task["wx.%d" % h] = wx_copy(h)
            task["wx.%d" % (2 + h)] = wx_quant(h)
            task["out0.%d" % h] = out0(0, h)
        for b in range(2):
            for h in range(2):
                task["x%d.%d" % (b, h)] = x_copy(b, h)
                task["xq%d.%d" % (b, h)] = x_quant(b, h)
            for v in range(2):
                task["dz2.%d%d" % (b, v)] = dz2(b, v)
                task["dz2q.%d%d" % (b, v)] = dz2_quant(b, v)
        for it in range(4):
            task["out1.%d" % it] = out1(it)

        task["hx0"] = lambda: (hx_transposes(0), weights(0))
        task["hx1"] = lambda: hx_transposes(1)
        task["g0"] = lambda: g_transposes(0)
        task["g1"] = lambda: g_transposes(1)
        for name in PROLOGUE:
            task[name]()

        for n in range(len(ORDER)):
            d = weights(n + 1) if n + 1 < len(ORDER) else {}
            if n == 1:
                load_sc(2)
                load_sp(3, ((0, 128),))
            elif n == 2:
                load_sc(3)
                raws["x0"] = load_x(0)
            elif n == 3:
                raws["x1"] = load_x(1)
            elif n == 5:
                raws["wx"] = load_wx()
            for r in range(NT):
                term(n, r)
                for k, name in PLAN[n]:
                    if k == r:
                        task[name]()
                for step in d.get(r, ()):
                    step()
                if r == 1:
                    silu_second(n)
                if r == SUM_AT:
                    if n > 0:
                        sum_transposes(n - 1)
                    if n + 2 < len(ORDER):
                        hx_transposes(n + 2)
                if r == SUM_AT + 1:
                    if n > 0:
                        dz_final(n - 1)
                    hx_square(n)
                if n > 0 and r == SUM_AT + 2:
                    dz_quant(n - 1)

        for a in (0, 2):
            task["sum%d" % a] = lambda a=a: sum_transposes(7, (a, a + 1))
            task["fin%d" % a] = lambda a=a: dz_final(7, (a, a + 1))
        task["dzq"] = lambda: dz_quant(7)
        for j in range(4):
            task["mm%d" % j] = out0_flat(1, j)
            task["tr%d" % j] = out0_turn(1, j)
        task["store"] = lambda: out0_store(1)
        for name in TAIL:
            task[name]()
